import numpy as np
import ml_dtypes


def mxq(x, axis, fmt="e4m3"):
    dtype, down = {"e4m3": (ml_dtypes.float8_e4m3fn, 7), "e5m2": (ml_dtypes.float8_e5m2, 14)}[fmt]
    v = np.moveaxis(np.asarray(x, np.float32).astype(ml_dtypes.bfloat16).astype(np.float64), axis, -1)
    blocks = v.reshape(v.shape[:-1] + (-1, 32))
    amax = np.abs(blocks).max(-1, keepdims=True)
    byte = np.maximum(np.where(amax > 0, np.frexp(amax)[1] - 1 + 127, 0) - down, 1)
    scale = np.exp2(byte - 127.0)
    codes = (blocks / scale).astype(np.float32).astype(dtype).astype(np.float64)
    return np.moveaxis((codes * scale).reshape(v.shape), -1, axis)


WIDE = False


def mx_kscale(k):
    if not WIDE:
        return np.ones(k)
    levels = np.array([10, -10, 5, -5, 0])
    if k % 512:
        return np.exp2(np.random.permutation(np.resize(levels, k // 32))).repeat(32)
    a = np.empty((k // 512, 16))
    for p in range(k // 512):
        a[p, :8] = np.random.permutation(np.resize(levels, 8))
        for g in range(8):
            far = levels[np.abs(levels - a[p, g]) >= 10]
            a[p, g + 8] = far[np.random.randint(len(far))]
    return np.exp2(a.ravel()).repeat(32)


BF16 = ml_dtypes.bfloat16


def bf(x):
    return np.asarray(x, np.float32).astype(BF16)


def f64(x):
    return np.asarray(x).astype(np.float64)


B, L_IMG, L_TXT, DM, H, D = 1, 6144, 2048, 512, 2, 64
L = L_TXT + L_IMG
HD = H * D
EPS = 1e-6


def rms(x, gain):
    return x / np.sqrt(np.mean(np.square(x), axis=-1, keepdims=True) + EPS) * gain


def qkv(x, w, qn, kn):
    y = (mxq(x, 2, "e4m3") @ mxq(w, 0, "e4m3")).reshape(x.shape[0], x.shape[1], 3, H, D)
    return rms(y[:, :, 0], qn), rms(y[:, :, 1], kn), y[:, :, 2]


def rope(x, fc):
    x_ = x.reshape(x.shape[:-1] + (D // 2, 1, 2))
    out = fc[:, None, :, :, 0] * x_[..., 0] + fc[:, None, :, :, 1] * x_[..., 1]
    return out.reshape(x.shape)


def setup_inputs():
    s = mx_kscale(DM)
    r = np.random.standard_normal
    return {
        "hidden_states": bf(r((B, L_IMG, DM)) * s),
        "encoder_hidden_states": bf(r((B, L_TXT, DM)) * s),
        "image_rotary_emb": bf(r((L, D // 2, 4)) * 0.6),
        "W_iqkv": bf(r((DM, 3 * HD)) / np.sqrt(DM) / s[:, None]),
        "W_eqkv": bf(r((DM, 3 * HD)) / np.sqrt(DM) / s[:, None]),
        "qn_scale": bf(1.0 + 0.1 * r(D)),
        "kn_scale": bf(1.0 + 0.1 * r(D)),
        "eqn_scale": bf(1.0 + 0.1 * r(D)),
        "ekn_scale": bf(1.0 + 0.1 * r(D)),
    }


def reference(hidden_states, encoder_hidden_states, image_rotary_emb, W_iqkv, W_eqkv, qn_scale, kn_scale, eqn_scale, ekn_scale):
    q, k, v = qkv(f64(hidden_states), f64(W_iqkv), f64(qn_scale), f64(kn_scale))
    eq, ek, ev = qkv(f64(encoder_hidden_states), f64(W_eqkv), f64(eqn_scale), f64(ekn_scale))
    q = np.concatenate((eq, q), axis=1)
    k = np.concatenate((ek, k), axis=1)
    v = np.concatenate((ev, v), axis=1)
    fc = f64(image_rotary_emb).reshape(L, D // 2, 2, 2)
    return rope(q, fc).reshape(B, L, HD), rope(k, fc).reshape(B, L, HD), v.reshape(B, L, HD)

@@ -1,0 +1,385 @@
+from contextlib import ExitStack
+
+import concourse.mybir as mybir
+from concourse.masks import make_identity
+
+FLOPS = 2 * 8192 * 512 * 384
+
+F32 = mybir.dt.float32
+BF16 = mybir.dt.bfloat16
+U32 = mybir.dt.uint32
+U8 = mybir.dt.uint8
+FP8X4 = mybir.dt.float8_e4m3fn_x4
+ALU = mybir.AluOpType
+ACT = mybir.ActivationFunctionType
+
+P = 128
+EPS = 1e-6
+GROUP_TILES = 8
+N_GROUPS = 8
+TEXT_GROUPS = 2
+UNIT_TILES = 2
+N_UNITS = 32
+CHUNK_TILES = 4
+N_CHUNKS = 16
+VECTOR_ADD_CHUNKS = (0, 2, 5, 8, 11, 14, 15)
+ACCUM_UNITS = (6, 10, 14, 18, 22, 26, 30)
+GAINS_AT_START = 8
+
+
+def tile_fluxattention_pa_t_kernel(
+    tc,
+    hidden_states,
+    encoder_hidden_states,
+    image_rotary_emb,
+    W_iqkv,
+    W_eqkv,
+    qn_scale,
+    kn_scale,
+    eqn_scale,
+    ekn_scale,
+    out_0,
+    out_1,
+    out_2,
+):
+    nc = tc.nc
+    x_img = hidden_states.flatten_outer_dims()
+    x_txt = encoder_hidden_states.flatten_outer_dims()
+    rot = image_rotary_emb.rearrange("l i f -> l (i f)")
+    outs = [out_0.flatten_outer_dims(), out_1.flatten_outer_dims(), out_2.flatten_outer_dims()]
+
+    with ExitStack() as ctx:
+        ctx.enter_context(tc.manual_schedule())
+        const = ctx.enter_context(tc.tile_pool(name="const", bufs=1))
+        xpool = ctx.enter_context(tc.tile_pool(name="xpool", bufs=N_CHUNKS))
+        fpool = ctx.enter_context(tc.tile_pool(name="fpool", bufs=N_GROUPS))
+        fgpool = ctx.enter_context(tc.tile_pool(name="fgpool", bufs=4))
+        sqpool = ctx.enter_context(tc.tile_pool(name="sqpool", bufs=3))
+        gpool = ctx.enter_context(tc.tile_pool(name="gpool", bufs=3))
+        cpool = ctx.enter_context(tc.tile_pool(name="cpool", bufs=3))
+        ppool = ctx.enter_context(tc.tile_pool(name="ppool", bufs=3))
+        opool = ctx.enter_context(tc.tile_pool(name="opool", bufs=4))
+        stat = ctx.enter_context(tc.tile_pool(name="stat", bufs=4))
+        tpsum = ctx.enter_context(tc.psum_pool(name="tpsum", bufs=2))
+        qkpsum = ctx.enter_context(tc.psum_pool(name="qkpsum", bufs=4))
+        vpsum = ctx.enter_context(tc.psum_pool(name="vpsum", bufs=2))
+
+        def chunk_rows(dram, c, lo, hi):
+            grp, half = divmod(c, 2)
+            return dram[1024 * grp : 1024 * grp + 1024, :].rearrange("(p t) f -> p t f", t=GROUP_TILES)[
+                :, 4 * half + lo : 4 * half + hi, :
+            ]
+
+        def load_gain(g, name):
+            raw = const.tile([P, 64], BF16, name=name + "_raw")
+            nc.scalar.dma_start(out=raw[:], in_=g.partition_broadcast(P))
+            return raw
+
+        def load_w(w, name):
+            raw = const.tile([P, 4, 384], BF16, name=name + "_raw")
+            nc.sync.dma_start(out=raw[:], in_=w.rearrange("(p t) c -> p t c", t=4))
+            return raw
+
+        def load_x(c, pieces):
+            if c < 2 * TEXT_GROUPS:
+                src, cc = x_txt, c
+            else:
+                src, cc = x_img, c - 2 * TEXT_GROUPS
+            xt = xpool.tile([P, CHUNK_TILES, 512], BF16, name="x")
+            step = CHUNK_TILES // pieces
+            for k in range(pieces):
+                nc.sync.dma_start(
+                    out=xt[:, step * k : step * k + step, :], in_=chunk_rows(src, cc, step * k, step * k + step)
+                )
+            return xt
+
+        def load_f(grp):
+            ft = fpool.tile([P, GROUP_TILES, 128], BF16, name="f")
+            nc.sync.dma_start(
+                out=ft[:],
+                in_=rot[1024 * grp : 1024 * grp + 1024, :].rearrange("(p t) f -> p t f", t=GROUP_TILES),
+            )
+            return ft
+
+        g_raw = [
+            [load_gain(eqn_scale, "eq"), load_gain(ekn_scale, "ek")],
+            [load_gain(qn_scale, "iq"), load_gain(kn_scale, "ik")],
+        ]
+        x_tiles = {}
+        f_tiles = {}
+        w_raw = {}
+        w_raw[0] = load_w(W_eqkv, "we")
+        x_tiles[0] = load_x(0, 2)
+        f_tiles[0] = load_f(0)
+        x_tiles[1] = load_x(1, 1)
+        w_raw[1] = load_w(W_iqkv, "wi")
+        f_tiles[1] = load_f(1)
+        for c in range(2, N_CHUNKS):
+            x_tiles[c] = load_x(c, 1)
+            if c < N_GROUPS:
+                f_tiles[c] = load_f(c)
+
+        ident = const.tile([P, P], F32, name="ident")
+        make_identity(nc, ident[:])
+        warm = const.tile([P, 1], F32, name="warm")
+        nc.vector.memset(warm[:], 1.0)
+        nc.scalar.activation(out=warm[:], in_=warm[:], func=ACT.Abs_reciprocal_sqrt)
+        junk = const.tile([P, 64], F32, name="junk")
+
+        def regroup_w(raw, name, copy):
+            grouped = const.tile([P, 384, 4], BF16, name=name + "_grouped", align_bytes=64)
+            for b in range(2):
+                copy(
+                    out=grouped[:, 0:256, :].rearrange("p (g b i) t -> p g b i t", g=4, b=2, i=32)[:, :, b],
+                    in_=raw[:, :, 0:256].rearrange("p t (g i b) -> p g b i t", g=4, i=32, b=2)[:, :, b],
+                )
+            copy(out=grouped[:, 256:384, :], in_=raw[:, :, 256:384].rearrange("p t n -> p n t"))
+            return grouped
+
+        def quantise_w(grouped, name):
+            codes = const.tile([P, 384], U32, name=name + "_codes", align_bytes=64)
+            scales = const.tile([P, 384], U8, name=name + "_scales", align_bytes=64)
+            for lo, hi in ((0, 256), (256, 384)):
+                nc.vector.quantize_mx(
+                    out=codes[:, lo:hi].bitcast(FP8X4),
+                    scales=scales[:, lo:hi],
+                    in_=grouped[:, lo:hi, :].rearrange("p n t -> p (n t)"),
+                )
+            return codes, scales
+
+        def expand_gain(raw, name):
+            gx = const.tile([P, 2, 32, 2], BF16, name=name + "_gx")
+            nc.vector.tensor_copy(
+                out=gx[:],
+                in_=raw[:].rearrange("p (i b) -> p b i", b=2).unsqueeze(3).to_broadcast([P, 2, 32, 2]),
+            )
+            return gx
+
+        fg_tiles = {}
+
+        def gain_rotary(m):
+            c, q = divmod(m, 2)
+            grp, half = divmod(c, 2)
+            s = 0 if grp < TEXT_GROUPS else 1
+            if m % 4 == 0:
+                fg_new = fgpool.tile([P, GROUP_TILES, 2, 128], F32, name="fg")
+                fg_tiles[grp] = fg_new
+            tiles = slice(4 * half, 4 * half + 4)
+            nc.gpsimd.tensor_tensor(
+                out=fg_tiles[grp][:, tiles, q, :].rearrange("p n (b c) -> p n b c", b=2),
+                in0=f_tiles[grp][:, tiles, :].rearrange("p n (c b) -> p n b c", b=2),
+                in1=g_x[s][q][:]
+                .rearrange("p b i a -> p b (i a)")
+                .unsqueeze(1)
+                .to_broadcast([P, CHUNK_TILES, 2, 64]),
+                op=ALU.mult,
+            )
+
+        xt_tiles = {}
+        xg_tiles = {}
+        xq_tiles = {}
+        qk_tiles = {}
+        v_tiles = {}
+        sq_tiles = {}
+        ssq_tiles = {}
+        rstd_tiles = {}
+        prod_tiles = {}
+        o_tiles = {}
+        vsb_tiles = {}
+
+        def valid(u):
+            return 0 <= u < N_UNITS
+
+        def stage_transpose(u):
+            if not valid(u):
+                return
+            xw = x_tiles[u // 2][:].bitcast(F32)
+            xt = tpsum.tile([P, 2, 2, 128], F32, name="xt")
+            xt_tiles[u] = xt
+            for a in range(2):
+                for half in range(2):
+                    nc.tensor.transpose(
+                        xt[:, a, half, :], xw[:, 2 * (u % 2) + a, half : 256 : 2], ident[:]
+                    )
+
+        def stage_copy(u):
+            if not valid(u):
+                return
+            if u % 2 == 0:
+                xg_new = gpool.tile([P, 2048], BF16, name="xg", align_bytes=64)
+                xg_tiles[u // 2] = xg_new
+            xg = xg_tiles[u // 2]
+            nc.scalar.copy(
+                out=xg[:, 1024 * (u % 2) : 1024 * (u % 2) + 1024]
+                .bitcast(F32)
+                .rearrange("p (a r h) -> p a r h", a=2, r=128, h=2),
+                in_=xt_tiles[u][:].rearrange("p a h r -> p a r h"),
+            )
+
+        def stage_quantise(c):
+            if not 0 <= c < N_CHUNKS:
+                return
+            xc = cpool.tile([P, 512], U32, name="xc", align_bytes=64)
+            xs = cpool.tile([P, 512], U8, name="xs", align_bytes=64)
+            nc.vector.quantize_mx(out=xc[:].bitcast(FP8X4), scales=xs[:], in_=xg_tiles[c][:])
+            xq_tiles[c] = (xc, xs)
+
+        def stage_matmul(u):
+            if not valid(u):
+                return
+            wc, ws = w_q[0 if u < 4 * TEXT_GROUPS else 1]
+            xc, xs = xq_tiles[u // 2]
+            vps = vpsum.tile([P, 2, 128], F32, name="vps")
+            v_tiles[u] = vps
+            qk = qkpsum.tile([P, 2, 256], F32, name="qk")
+            qk_tiles[u] = qk
+            for a in range(2):
+                cols = slice(256 * (u % 2) + 128 * a, 256 * (u % 2) + 128 * a + 128)
+                nc.tensor.matmul_mx(
+                    out=qk[:, a, :],
+                    lhsT=xc[:, cols].bitcast(FP8X4),
+                    lhsT_scale=xs[:, cols],
+                    rhs=wc[:, 0:256].bitcast(FP8X4),
+                    rhs_scale=ws[:, 0:256],
+                    start=True,
+                    stop=True,
+                )
+                nc.tensor.matmul_mx(
+                    out=vps[:, a, :],
+                    lhsT=xc[:, cols].bitcast(FP8X4),
+                    lhsT_scale=xs[:, cols],
+                    rhs=wc[:, 256:384].bitcast(FP8X4),
+                    rhs_scale=ws[:, 256:384],
+                    start=True,
+                    stop=True,
+                )
+
+        def stage_square(u):
+            if not valid(u):
+                return
+            if u in ACCUM_UNITS:
+                ssq = stat.tile([P, 8], F32, name="ssq")
+                ssq_tiles[u] = ssq
+                for j in range(8):
+                    nc.scalar.activation(
+                        out=junk[:],
+                        in_=qk_tiles[u][:, j // 4, 64 * (j % 4) : 64 * (j % 4) + 64],
+                        func=ACT.Square,
+                        accum_out=ssq[:, j : j + 1],
+                    )
+                return
+            sq = sqpool.tile([P, 512], F32, name="sq")
+            sq_tiles[u] = sq
+            nc.scalar.activation(out=sq[:], in_=qk_tiles[u][:].rearrange("p a c -> p (a c)"), func=ACT.Square)
+
+        def stage_v(u):
+            if not valid(u):
+                return
+            if u % 2 == 0:
+                vsb_new = opool.tile([P, CHUNK_TILES, 128], F32, name="vsb")
+                vsb_tiles[u // 2] = vsb_new
+            vsb = vsb_tiles[u // 2]
+            nc.scalar.copy(out=vsb[:, 2 * (u % 2) : 2 * (u % 2) + 2, :], in_=v_tiles[u][:])
+            if u % 2 == 1:
+                nc.sync.dma_start(out=chunk_rows(outs[2], u // 2, 0, CHUNK_TILES), in_=vsb[:])
+
+        def stage_reduce(u):
+            if not valid(u) or u in ACCUM_UNITS:
+                return
+            ssq = stat.tile([P, 8], F32, name="ssq")
+            ssq_tiles[u] = ssq
+            nc.vector.tensor_reduce(
+                out=ssq[:],
+                in_=sq_tiles[u][:].rearrange("p (g c) -> p g c", c=64),
+                axis=mybir.AxisListType.X,
+                op=ALU.add,
+            )
+
+        def stage_rstd(u):
+            if not valid(u):
+                return
+            rstd = stat.tile([P, 8], F32, name="rstd")
+            nc.scalar.activation(
+                out=rstd[:], in_=ssq_tiles[u][:], func=ACT.Abs_reciprocal_sqrt, scale=1.0 / 64.0, bias=EPS
+            )
+            rstd_tiles[u] = rstd
+
+        def stage_products(u):
+            if not valid(u):
+                return
+            grp, t0 = divmod(2 * u, GROUP_TILES)
+            if u % 2 == 0:
+                prod_new = ppool.tile([P, 2, CHUNK_TILES, 2, 128], F32, name="prod")
+                prod_tiles[u // 2] = prod_new
+            prod = prod_tiles[u // 2]
+            for t in range(2):
+                for g in range(4):
+                    q, h = divmod(g, 2)
+                    nc.vector.scalar_tensor_tensor(
+                        out=prod[:, q, 2 * (u % 2) + t, h, :].rearrange("p (c a) -> p c a", a=2),
+                        in0=qk_tiles[u][:, t, 64 * g : 64 * g + 64].unsqueeze(2).to_broadcast([P, 64, 2]),
+                        scalar=rstd_tiles[u][:, 4 * t + g : 4 * t + g + 1],
+                        in1=fg_tiles[grp][:, t0 + t, q, :].rearrange("p (c a) -> p c a", a=2),
+                        op0=ALU.mult,
+                        op1=ALU.mult,
+                    )
+
+        def add_halves(eng, c, lo, hi):
+            pv = prod_tiles[c][:, :, lo:hi].rearrange("p q t h (b c) -> p q (t h) b c", b=2)
+            eng.tensor_tensor(
+                out=o_tiles[c][:, :, lo:hi, :].rearrange("p q t (h c) -> p q (t h) c", h=2),
+                in0=pv[:, :, :, 0, :],
+                in1=pv[:, :, :, 1, :],
+                op=ALU.add,
+            )
+
+        def store_qk(c):
+            nc.sync.dma_start(out=chunk_rows(outs[0], c, 0, CHUNK_TILES), in_=o_tiles[c][:, 0])
+            nc.sync.dma_start(out=chunk_rows(outs[1], c, 0, CHUNK_TILES), in_=o_tiles[c][:, 1])
+
+        def stage_add_vector(c):
+            if not 0 <= c < N_CHUNKS or c not in VECTOR_ADD_CHUNKS:
+                return
+            o_new = opool.tile([P, 2, CHUNK_TILES, 128], F32, name="o")
+            o_tiles[c] = o_new
+            add_halves(nc.vector, c, 0, CHUNK_TILES)
+            store_qk(c)
+
+        def stage_add_gpsimd(u):
+            if not valid(u) or u // 2 in VECTOR_ADD_CHUNKS:
+                return
+            if u % 2 == 0:
+                o_new = opool.tile([P, 2, CHUNK_TILES, 128], F32, name="o")
+                o_tiles[u // 2] = o_new
+            add_halves(nc.gpsimd, u // 2, 2 * (u % 2), 2 * (u % 2) + 2)
+            if u % 2 == 1:
+                store_qk(u // 2)
+
+        g_x = [
+            [expand_gain(g_raw[0][0], "eq"), expand_gain(g_raw[0][1], "ek")],
+            [expand_gain(g_raw[1][0], "iq"), expand_gain(g_raw[1][1], "ik")],
+        ]
+        w_q = {}
+        w_q[0] = quantise_w(regroup_w(w_raw[0], "we", nc.vector.tensor_copy), "we")
+        w_grouped = {}
+        for m in range(GAINS_AT_START):
+            gain_rotary(m)
+        for i in range(-6, N_UNITS + 3):
+            stage_rstd(i)
+            stage_copy(i + 5)
+            stage_transpose(i + 6)
+            stage_square(i + 2)
+            stage_v(i + 2)
+            stage_products(i - 1)
+            stage_reduce(i + 1)
+            if i % 2 == 1:
+                stage_quantise((i + 3) // 2)
+                stage_add_vector((i - 3) // 2)
+            stage_matmul(i + 3)
+            stage_add_gpsimd(i - 1)
+            if i == 1:
+                w_grouped[1] = regroup_w(w_raw[1], "wi", nc.scalar.copy)
+            if i == 3:
+                w_q[1] = quantise_w(w_grouped[1], "wi")
+            if GAINS_AT_START <= i + 6 < 2 * N_CHUNKS:
+                gain_rotary(i + 6)

@@ -18,13 +18,9 @@ EPS = 1e-6
 GROUP_TILES = 8
 N_GROUPS = 8
 TEXT_GROUPS = 2
-UNIT_TILES = 2
 N_UNITS = 32
 CHUNK_TILES = 4
 N_CHUNKS = 16
-VECTOR_ADD_CHUNKS = (0, 2, 5, 8, 11, 14, 15)
-ACCUM_UNITS = (6, 10, 14, 18, 22, 26, 30)
-GAINS_AT_START = 8
 
 
 def tile_fluxattention_pa_t_kernel(
@@ -53,15 +49,15 @@ def tile_fluxattention_pa_t_kernel(
         const = ctx.enter_context(tc.tile_pool(name="const", bufs=1))
         xpool = ctx.enter_context(tc.tile_pool(name="xpool", bufs=N_CHUNKS))
         fpool = ctx.enter_context(tc.tile_pool(name="fpool", bufs=N_GROUPS))
-        fgpool = ctx.enter_context(tc.tile_pool(name="fgpool", bufs=4))
-        sqpool = ctx.enter_context(tc.tile_pool(name="sqpool", bufs=3))
         gpool = ctx.enter_context(tc.tile_pool(name="gpool", bufs=3))
-        cpool = ctx.enter_context(tc.tile_pool(name="cpool", bufs=3))
+        cpool = ctx.enter_context(tc.tile_pool(name="cpool", bufs=4))
+        zpool = ctx.enter_context(tc.tile_pool(name="zpool", bufs=3))
         ppool = ctx.enter_context(tc.tile_pool(name="ppool", bufs=3))
         opool = ctx.enter_context(tc.tile_pool(name="opool", bufs=4))
         stat = ctx.enter_context(tc.tile_pool(name="stat", bufs=4))
         tpsum = ctx.enter_context(tc.psum_pool(name="tpsum", bufs=2))
-        qkpsum = ctx.enter_context(tc.psum_pool(name="qkpsum", bufs=4))
+        ypsum = ctx.enter_context(tc.psum_pool(name="ypsum", bufs=2))
+        zpsum = ctx.enter_context(tc.psum_pool(name="zpsum", bufs=2))
         vpsum = ctx.enter_context(tc.psum_pool(name="vpsum", bufs=2))
 
         def chunk_rows(dram, c, lo, hi):
@@ -69,11 +65,6 @@ def tile_fluxattention_pa_t_kernel(
             return dram[1024 * grp : 1024 * grp + 1024, :].rearrange("(p t) f -> p t f", t=GROUP_TILES)[
                 :, 4 * half + lo : 4 * half + hi, :
             ]
-
-        def load_gain(g, name):
-            raw = const.tile([P, 64], BF16, name=name + "_raw")
-            nc.scalar.dma_start(out=raw[:], in_=g.partition_broadcast(P))
-            return raw
 
         def load_w(w, name):
             raw = const.tile([P, 4, 384], BF16, name=name + "_raw")
@@ -101,17 +92,18 @@ def tile_fluxattention_pa_t_kernel(
             )
             return ft
 
-        g_raw = [
-            [load_gain(eqn_scale, "eq"), load_gain(ekn_scale, "ek")],
-            [load_gain(qn_scale, "iq"), load_gain(kn_scale, "ik")],
-        ]
+        gain_rows = const.tile([P, 64], BF16, name="gain_rows")
+        nc.vector.memset(gain_rows[:], 0.0)
+
         x_tiles = {}
         f_tiles = {}
         w_raw = {}
         w_raw[0] = load_w(W_eqkv, "we")
         x_tiles[0] = load_x(0, 2)
-        f_tiles[0] = load_f(0)
+        for j, g in enumerate((eqn_scale, ekn_scale, qn_scale, kn_scale)):
+            nc.sync.dma_start(out=gain_rows[j : j + 1, :], in_=g.rearrange("(o d) -> o d", o=1))
         x_tiles[1] = load_x(1, 1)
+        f_tiles[0] = load_f(0)
         w_raw[1] = load_w(W_iqkv, "wi")
         f_tiles[1] = load_f(1)
         for c in range(2, N_CHUNKS):
@@ -121,10 +113,15 @@ def tile_fluxattention_pa_t_kernel(
 
         ident = const.tile([P, P], F32, name="ident")
         make_identity(nc, ident[:])
+        ident_bf = const.tile([P, P], BF16, name="ident_bf")
+        make_identity(nc, ident_bf[:])
         warm = const.tile([P, 1], F32, name="warm")
         nc.vector.memset(warm[:], 1.0)
         nc.scalar.activation(out=warm[:], in_=warm[:], func=ACT.Abs_reciprocal_sqrt)
-        junk = const.tile([P, 64], F32, name="junk")
+        head_ones = const.tile([P, 2], F32, name="head_ones")
+        nc.vector.memset(head_ones[:], 0.0)
+        nc.vector.memset(head_ones[0:64, 0:1], 1.0)
+        nc.vector.memset(head_ones[64:128, 1:2], 1.0)
 
         def regroup_w(raw, name, copy):
             grouped = const.tile([P, 384, 4], BF16, name=name + "_grouped", align_bytes=64)
@@ -147,41 +144,14 @@ def tile_fluxattention_pa_t_kernel(
                 )
             return codes, scales
 
-        def expand_gain(raw, name):
-            gx = const.tile([P, 2, 32, 2], BF16, name=name + "_gx")
-            nc.vector.tensor_copy(
-                out=gx[:],
-                in_=raw[:].rearrange("p (i b) -> p b i", b=2).unsqueeze(3).to_broadcast([P, 2, 32, 2]),
-            )
-            return gx
-
-        fg_tiles = {}
-
-        def gain_rotary(m):
-            c, q = divmod(m, 2)
-            grp, half = divmod(c, 2)
-            s = 0 if grp < TEXT_GROUPS else 1
-            if m % 4 == 0:
-                fg_new = fgpool.tile([P, GROUP_TILES, 2, 128], F32, name="fg")
-                fg_tiles[grp] = fg_new
-            tiles = slice(4 * half, 4 * half + 4)
-            nc.gpsimd.tensor_tensor(
-                out=fg_tiles[grp][:, tiles, q, :].rearrange("p n (b c) -> p n b c", b=2),
-                in0=f_tiles[grp][:, tiles, :].rearrange("p n (c b) -> p n b c", b=2),
-                in1=g_x[s][q][:]
-                .rearrange("p b i a -> p b (i a)")
-                .unsqueeze(1)
-                .to_broadcast([P, CHUNK_TILES, 2, 64]),
-                op=ALU.mult,
-            )
-
         xt_tiles = {}
         xg_tiles = {}
         xq_tiles = {}
-        qk_tiles = {}
-        v_tiles = {}
+        yt_tiles = {}
+        zt_tiles = {}
         sq_tiles = {}
-        ssq_tiles = {}
+        z_tiles = {}
+        vs_tiles = {}
         rstd_tiles = {}
         prod_tiles = {}
         o_tiles = {}
@@ -198,9 +168,7 @@ def tile_fluxattention_pa_t_kernel(
             xt_tiles[u] = xt
             for a in range(2):
                 for half in range(2):
-                    nc.tensor.transpose(
-                        xt[:, a, half, :], xw[:, 2 * (u % 2) + a, half : 256 : 2], ident[:]
-                    )
+                    nc.tensor.transpose(xt[:, a, half, :], xw[:, 2 * (u % 2) + a, half : 256 : 2], ident[:])
 
         def stage_copy(u):
             if not valid(u):
@@ -209,7 +177,8 @@ def tile_fluxattention_pa_t_kernel(
                 xg_new = gpool.tile([P, 2048], BF16, name="xg", align_bytes=64)
                 xg_tiles[u // 2] = xg_new
             xg = xg_tiles[u // 2]
-            nc.scalar.copy(
+            copy = nc.scalar.copy if u % 2 == 0 else nc.vector.tensor_copy
+            copy(
                 out=xg[:, 1024 * (u % 2) : 1024 * (u % 2) + 1024]
                 .bitcast(F32)
                 .rearrange("p (a r h) -> p a r h", a=2, r=128, h=2),
@@ -224,28 +193,36 @@ def tile_fluxattention_pa_t_kernel(
             nc.vector.quantize_mx(out=xc[:].bitcast(FP8X4), scales=xs[:], in_=xg_tiles[c][:])
             xq_tiles[c] = (xc, xs)
 
-        def stage_matmul(u):
+        def stage_matmul_qk(u):
             if not valid(u):
                 return
             wc, ws = w_q[0 if u < 4 * TEXT_GROUPS else 1]
             xc, xs = xq_tiles[u // 2]
-            vps = vpsum.tile([P, 2, 128], F32, name="vps")
-            v_tiles[u] = vps
-            qk = qkpsum.tile([P, 2, 256], F32, name="qk")
-            qk_tiles[u] = qk
-            for a in range(2):
-                cols = slice(256 * (u % 2) + 128 * a, 256 * (u % 2) + 128 * a + 128)
+            yt = ypsum.tile([P, 2, 256], F32, name="yt")
+            yt_tiles[u] = yt
+            cols = slice(256 * (u % 2), 256 * (u % 2) + 256)
+            for q in range(2):
                 nc.tensor.matmul_mx(
-                    out=qk[:, a, :],
-                    lhsT=xc[:, cols].bitcast(FP8X4),
-                    lhsT_scale=xs[:, cols],
-                    rhs=wc[:, 0:256].bitcast(FP8X4),
-                    rhs_scale=ws[:, 0:256],
+                    out=yt[:, q, :],
+                    lhsT=wc[:, 128 * q : 128 * q + 128].bitcast(FP8X4),
+                    lhsT_scale=ws[:, 128 * q : 128 * q + 128],
+                    rhs=xc[:, cols].bitcast(FP8X4),
+                    rhs_scale=xs[:, cols],
                     start=True,
                     stop=True,
                 )
+
+        def stage_matmul_v(u):
+            if not valid(u):
+                return
+            wc, ws = w_q[0 if u < 4 * TEXT_GROUPS else 1]
+            xc, xs = xq_tiles[u // 2]
+            vs = vpsum.tile([P, 264], F32, name="vs")
+            vs_tiles[u] = vs
+            for a in range(2):
+                cols = slice(256 * (u % 2) + 128 * a, 256 * (u % 2) + 128 * a + 128)
                 nc.tensor.matmul_mx(
-                    out=vps[:, a, :],
+                    out=vs[:, 128 * a : 128 * a + 128],
                     lhsT=xc[:, cols].bitcast(FP8X4),
                     lhsT_scale=xs[:, cols],
                     rhs=wc[:, 256:384].bitcast(FP8X4),
@@ -254,55 +231,58 @@ def tile_fluxattention_pa_t_kernel(
                     stop=True,
                 )
 
-        def stage_square(u):
+        def stage_gain_square(u):
             if not valid(u):
                 return
-            if u in ACCUM_UNITS:
-                ssq = stat.tile([P, 8], F32, name="ssq")
-                ssq_tiles[u] = ssq
-                for j in range(8):
-                    nc.scalar.activation(
-                        out=junk[:],
-                        in_=qk_tiles[u][:, j // 4, 64 * (j % 4) : 64 * (j % 4) + 64],
-                        func=ACT.Square,
-                        accum_out=ssq[:, j : j + 1],
-                    )
-                return
-            sq = sqpool.tile([P, 512], F32, name="sq")
+            s = 0 if u < 4 * TEXT_GROUPS else 1
+            zt = zpool.tile([P, 2, 256], F32, name="zt")
+            zt_tiles[u] = zt
+            sq = zpool.tile([P, 2, 256], F32, name="sq")
             sq_tiles[u] = sq
-            nc.scalar.activation(out=sq[:], in_=qk_tiles[u][:].rearrange("p a c -> p (a c)"), func=ACT.Square)
+            nc.scalar.activation(
+                out=sq[:].rearrange("p q r -> p (q r)"), in_=yt_tiles[u][:].rearrange("p q r -> p (q r)"), func=ACT.Square
+            )
+            for q in range(2):
+                nc.scalar.activation(
+                    out=zt[:, q, :], in_=yt_tiles[u][:, q, :], func=ACT.Copy, scale=gain_col[:, 2 * s + q : 2 * s + q + 1]
+                )
 
-        def stage_v(u):
+        def stage_back(u):
             if not valid(u):
                 return
-            if u % 2 == 0:
-                vsb_new = opool.tile([P, CHUNK_TILES, 128], F32, name="vsb")
-                vsb_tiles[u // 2] = vsb_new
-            vsb = vsb_tiles[u // 2]
-            nc.scalar.copy(out=vsb[:, 2 * (u % 2) : 2 * (u % 2) + 2, :], in_=v_tiles[u][:])
-            if u % 2 == 1:
-                nc.sync.dma_start(out=chunk_rows(outs[2], u // 2, 0, CHUNK_TILES), in_=vsb[:])
+            z = zpsum.tile([P, 2, 2, 128], F32, name="z")
+            z_tiles[u] = z
+            vs = vs_tiles[u]
+            for a in range(2):
+                for q in range(2):
+                    nc.tensor.matmul(
+                        out=vs[:, 256 + 4 * a + 2 * q : 256 + 4 * a + 2 * q + 2],
+                        lhsT=sq_tiles[u][:, q, 128 * a : 128 * a + 128],
+                        rhs=head_ones[:],
+                        start=True,
+                        stop=True,
+                    )
+            for a in range(2):
+                for q in range(2):
+                    nc.tensor.transpose(z[:, a, q, :], zt_tiles[u][:, q, 128 * a : 128 * a + 128], ident[:])
 
-        def stage_reduce(u):
-            if not valid(u) or u in ACCUM_UNITS:
-                return
-            ssq = stat.tile([P, 8], F32, name="ssq")
-            ssq_tiles[u] = ssq
-            nc.vector.tensor_reduce(
-                out=ssq[:],
-                in_=sq_tiles[u][:].rearrange("p (g c) -> p g c", c=64),
-                axis=mybir.AxisListType.X,
-                op=ALU.add,
-            )
-
-        def stage_rstd(u):
+        def stage_rstd_v(u):
             if not valid(u):
                 return
             rstd = stat.tile([P, 8], F32, name="rstd")
             nc.scalar.activation(
-                out=rstd[:], in_=ssq_tiles[u][:], func=ACT.Abs_reciprocal_sqrt, scale=1.0 / 64.0, bias=EPS
+                out=rstd[:], in_=vs_tiles[u][:, 256:264], func=ACT.Abs_reciprocal_sqrt, scale=1.0 / 64.0, bias=EPS
             )
             rstd_tiles[u] = rstd
+            if u % 2 == 0:
+                vsb_new = opool.tile([P, CHUNK_TILES, 128], F32, name="vsb")
+                vsb_tiles[u // 2] = vsb_new
+            vsb = vsb_tiles[u // 2]
+            nc.scalar.copy(
+                out=vsb[:, 2 * (u % 2) : 2 * (u % 2) + 2, :].rearrange("p a c -> p (a c)"), in_=vs_tiles[u][:, 0:256]
+            )
+            if u % 2 == 1:
+                nc.sync.dma_start(out=chunk_rows(outs[2], u // 2, 0, CHUNK_TILES), in_=vsb[:])
 
         def stage_products(u):
             if not valid(u):
@@ -312,74 +292,68 @@ def tile_fluxattention_pa_t_kernel(
                 prod_new = ppool.tile([P, 2, CHUNK_TILES, 2, 128], F32, name="prod")
                 prod_tiles[u // 2] = prod_new
             prod = prod_tiles[u // 2]
-            for t in range(2):
+            for a in range(2):
                 for g in range(4):
                     q, h = divmod(g, 2)
                     nc.vector.scalar_tensor_tensor(
-                        out=prod[:, q, 2 * (u % 2) + t, h, :].rearrange("p (c a) -> p c a", a=2),
-                        in0=qk_tiles[u][:, t, 64 * g : 64 * g + 64].unsqueeze(2).to_broadcast([P, 64, 2]),
-                        scalar=rstd_tiles[u][:, 4 * t + g : 4 * t + g + 1],
-                        in1=fg_tiles[grp][:, t0 + t, q, :].rearrange("p (c a) -> p c a", a=2),
+                        out=prod[:, q, 2 * (u % 2) + a, h, :].rearrange("p (b i e) -> p b i e", b=2, e=2),
+                        in0=z_tiles[u][:, a, q, 64 * h : 64 * h + 64]
+                        .rearrange("p (b i) -> p b i", b=2)
+                        .unsqueeze(3)
+                        .to_broadcast([P, 2, 32, 2]),
+                        scalar=rstd_tiles[u][:, 4 * a + g : 4 * a + g + 1],
+                        in1=f_tiles[grp][:, t0 + a, :].rearrange("p (i e b) -> p b i e", e=2, b=2),
                         op0=ALU.mult,
                         op1=ALU.mult,
                     )
 
-        def add_halves(eng, c, lo, hi):
-            pv = prod_tiles[c][:, :, lo:hi].rearrange("p q t h (b c) -> p q (t h) b c", b=2)
-            eng.tensor_tensor(
-                out=o_tiles[c][:, :, lo:hi, :].rearrange("p q t (h c) -> p q (t h) c", h=2),
+        def stage_add(u):
+            if not valid(u):
+                return
+            c = u // 2
+            if u % 2 == 0:
+                o_new = opool.tile([P, 2, CHUNK_TILES, 128], F32, name="o")
+                o_tiles[c] = o_new
+            lo = 2 * (u % 2)
+            pv = prod_tiles[c][:, :, lo : lo + 2].rearrange("p q t h (b c) -> p q (t h) b c", b=2)
+            nc.gpsimd.tensor_tensor(
+                out=o_tiles[c][:, :, lo : lo + 2, :].rearrange("p q t (h c) -> p q (t h) c", h=2),
                 in0=pv[:, :, :, 0, :],
                 in1=pv[:, :, :, 1, :],
                 op=ALU.add,
             )
-
-        def store_qk(c):
-            nc.sync.dma_start(out=chunk_rows(outs[0], c, 0, CHUNK_TILES), in_=o_tiles[c][:, 0])
-            nc.sync.dma_start(out=chunk_rows(outs[1], c, 0, CHUNK_TILES), in_=o_tiles[c][:, 1])
-
-        def stage_add_vector(c):
-            if not 0 <= c < N_CHUNKS or c not in VECTOR_ADD_CHUNKS:
-                return
-            o_new = opool.tile([P, 2, CHUNK_TILES, 128], F32, name="o")
-            o_tiles[c] = o_new
-            add_halves(nc.vector, c, 0, CHUNK_TILES)
-            store_qk(c)
-
-        def stage_add_gpsimd(u):
-            if not valid(u) or u // 2 in VECTOR_ADD_CHUNKS:
-                return
-            if u % 2 == 0:
-                o_new = opool.tile([P, 2, CHUNK_TILES, 128], F32, name="o")
-                o_tiles[u // 2] = o_new
-            add_halves(nc.gpsimd, u // 2, 2 * (u % 2), 2 * (u % 2) + 2)
             if u % 2 == 1:
-                store_qk(u // 2)
+                nc.sync.dma_start(out=chunk_rows(outs[0], c, 0, CHUNK_TILES), in_=o_tiles[c][:, 0])
+                nc.sync.dma_start(out=chunk_rows(outs[1], c, 0, CHUNK_TILES), in_=o_tiles[c][:, 1])
 
-        g_x = [
-            [expand_gain(g_raw[0][0], "eq"), expand_gain(g_raw[0][1], "ek")],
-            [expand_gain(g_raw[1][0], "iq"), expand_gain(g_raw[1][1], "ik")],
-        ]
         w_q = {}
         w_q[0] = quantise_w(regroup_w(w_raw[0], "we", nc.vector.tensor_copy), "we")
-        w_grouped = {}
-        for m in range(GAINS_AT_START):
-            gain_rotary(m)
-        for i in range(-6, N_UNITS + 3):
-            stage_rstd(i)
-            stage_copy(i + 5)
+        w_grouped_i = regroup_w(w_raw[1], "wi", nc.gpsimd.tensor_copy)
+        gain_col = const.tile([P, 4], F32, name="gain_col")
+
+        def gain_columns():
+            gain_perm = const.tile([P, 128], BF16, name="gain_perm")
+            nc.vector.tensor_copy(
+                out=gain_perm[:].rearrange("p (h b i) -> p h b i", h=2, b=2),
+                in_=gain_rows[:].rearrange("p (i b) -> p b i", b=2).unsqueeze(1).to_broadcast([P, 2, 2, 32]),
+            )
+            gain_ps = vpsum.tile([P, 128], BF16, name="vs")
+            nc.tensor.transpose(gain_ps[:], gain_perm[:], ident_bf[:])
+            nc.vector.tensor_copy(out=gain_col[:], in_=gain_ps[:, 0:4])
+
+        for i in range(-6, N_UNITS + 2):
+            stage_back(i)
             stage_transpose(i + 6)
-            stage_square(i + 2)
-            stage_v(i + 2)
+            stage_gain_square(i + 1)
             stage_products(i - 1)
-            stage_reduce(i + 1)
+            stage_copy(i + 5)
+            stage_rstd_v(i)
             if i % 2 == 1:
                 stage_quantise((i + 3) // 2)
-                stage_add_vector((i - 3) // 2)
-            stage_matmul(i + 3)
-            stage_add_gpsimd(i - 1)
+            stage_matmul_qk(i + 2)
+            stage_matmul_v(i + 1)
+            stage_add(i - 2)
+            if i == -5:
+                gain_columns()
             if i == 1:
-                w_grouped[1] = regroup_w(w_raw[1], "wi", nc.scalar.copy)
-            if i == 3:
-                w_q[1] = quantise_w(w_grouped[1], "wi")
-            if GAINS_AT_START <= i + 6 < 2 * N_CHUNKS:
-                gain_rotary(i + 6)
+                w_q[1] = quantise_w(w_grouped_i, "wi")

@@ -21,6 +21,7 @@ TEXT_GROUPS = 2
 N_UNITS = 32
 CHUNK_TILES = 4
 N_CHUNKS = 16
+SUM_COLS = 64
 
 
 def tile_fluxattention_pa_t_kernel(
@@ -118,7 +119,7 @@ def tile_fluxattention_pa_t_kernel(
         warm = const.tile([P, 1], F32, name="warm")
         nc.vector.memset(warm[:], 1.0)
         nc.scalar.activation(out=warm[:], in_=warm[:], func=ACT.Abs_reciprocal_sqrt)
-        head_ones = const.tile([P, 2], F32, name="head_ones")
+        head_ones = const.tile([P, SUM_COLS], F32, name="head_ones")
         nc.vector.memset(head_ones[:], 0.0)
         nc.vector.memset(head_ones[0:64, 0:1], 1.0)
         nc.vector.memset(head_ones[64:128, 1:2], 1.0)
@@ -217,7 +218,7 @@ def tile_fluxattention_pa_t_kernel(
                 return
             wc, ws = w_q[0 if u < 4 * TEXT_GROUPS else 1]
             xc, xs = xq_tiles[u // 2]
-            vs = vpsum.tile([P, 264], F32, name="vs")
+            vs = vpsum.tile([P, 256 + 4 * SUM_COLS], F32, name="vs")
             vs_tiles[u] = vs
             for a in range(2):
                 cols = slice(256 * (u % 2) + 128 * a, 256 * (u % 2) + 128 * a + 128)
@@ -256,7 +257,7 @@ def tile_fluxattention_pa_t_kernel(
             for a in range(2):
                 for q in range(2):
                     nc.tensor.matmul(
-                        out=vs[:, 256 + 4 * a + 2 * q : 256 + 4 * a + 2 * q + 2],
+                        out=vs[:, 256 + SUM_COLS * (2 * a + q) : 256 + SUM_COLS * (2 * a + q + 1)],
                         lhsT=sq_tiles[u][:, q, 128 * a : 128 * a + 128],
                         rhs=head_ones[:],
                         start=True,
@@ -271,7 +272,11 @@ def tile_fluxattention_pa_t_kernel(
                 return
             rstd = stat.tile([P, 8], F32, name="rstd")
             nc.scalar.activation(
-                out=rstd[:], in_=vs_tiles[u][:, 256:264], func=ACT.Abs_reciprocal_sqrt, scale=1.0 / 64.0, bias=EPS
+                out=rstd[:].rearrange("p (j h) -> p j h", h=2),
+                in_=vs_tiles[u][:, 256 : 256 + 4 * SUM_COLS].rearrange("p (j n) -> p j n", n=SUM_COLS)[:, :, 0:2],
+                func=ACT.Abs_reciprocal_sqrt,
+                scale=1.0 / 64.0,
+                bias=EPS,
             )
             rstd_tiles[u] = rstd
             if u % 2 == 0:

@@ -21,7 +21,7 @@ TEXT_GROUPS = 2
 N_UNITS = 32
 CHUNK_TILES = 4
 N_CHUNKS = 16
-SUM_COLS = 64
+SUM_COLS = 128
 
 
 def tile_fluxattention_pa_t_kernel(
@@ -93,7 +93,7 @@ def tile_fluxattention_pa_t_kernel(
             )
             return ft
 
-        gain_rows = const.tile([P, 64], BF16, name="gain_rows")
+        gain_rows = const.tile([P, 128], BF16, name="gain_rows")
         nc.vector.memset(gain_rows[:], 0.0)
 
         x_tiles = {}
@@ -102,7 +102,9 @@ def tile_fluxattention_pa_t_kernel(
         w_raw[0] = load_w(W_eqkv, "we")
         x_tiles[0] = load_x(0, 2)
         for j, g in enumerate((eqn_scale, ekn_scale, qn_scale, kn_scale)):
-            nc.sync.dma_start(out=gain_rows[j : j + 1, :], in_=g.rearrange("(o d) -> o d", o=1))
+            nc.sync.dma_start(
+                out=gain_rows[j // 2 : j // 2 + 1, 64 * (j % 2) : 64 * (j % 2) + 64], in_=g.rearrange("(o d) -> o d", o=1)
+            )
         x_tiles[1] = load_x(1, 1)
         f_tiles[0] = load_f(0)
         w_raw[1] = load_w(W_iqkv, "wi")
@@ -119,17 +121,17 @@ def tile_fluxattention_pa_t_kernel(
         warm = const.tile([P, 1], F32, name="warm")
         nc.vector.memset(warm[:], 1.0)
         nc.scalar.activation(out=warm[:], in_=warm[:], func=ACT.Abs_reciprocal_sqrt)
-        head_ones = const.tile([P, SUM_COLS], F32, name="head_ones")
-        nc.vector.memset(head_ones[:], 0.0)
-        nc.vector.memset(head_ones[0:64, 0:1], 1.0)
-        nc.vector.memset(head_ones[64:128, 1:2], 1.0)
+        group_ones = const.tile([P, SUM_COLS], F32, name="group_ones")
+        nc.vector.memset(group_ones[:], 0.0)
+        for g in range(4):
+            nc.vector.memset(group_ones[32 * g : 32 * g + 32, g : g + 1], 1.0)
 
         def regroup_w(raw, name, copy):
             grouped = const.tile([P, 384, 4], BF16, name=name + "_grouped", align_bytes=64)
             for b in range(2):
                 copy(
-                    out=grouped[:, 0:256, :].rearrange("p (g b i) t -> p g b i t", g=4, b=2, i=32)[:, :, b],
-                    in_=raw[:, :, 0:256].rearrange("p t (g i b) -> p g b i t", g=4, i=32, b=2)[:, :, b],
+                    out=grouped[:, 128 * b : 128 * b + 128, :],
+                    in_=raw[:, :, 0:256].rearrange("p t (c b) -> p b c t", b=2)[:, b],
                 )
             copy(out=grouped[:, 256:384, :], in_=raw[:, :, 256:384].rearrange("p t n -> p n t"))
             return grouped
@@ -151,6 +153,7 @@ def tile_fluxattention_pa_t_kernel(
         yt_tiles = {}
         zt_tiles = {}
         sq_tiles = {}
+        fold_tiles = {}
         z_tiles = {}
         vs_tiles = {}
         rstd_tiles = {}
@@ -202,11 +205,11 @@ def tile_fluxattention_pa_t_kernel(
             yt = ypsum.tile([P, 2, 256], F32, name="yt")
             yt_tiles[u] = yt
             cols = slice(256 * (u % 2), 256 * (u % 2) + 256)
-            for q in range(2):
+            for b in range(2):
                 nc.tensor.matmul_mx(
-                    out=yt[:, q, :],
-                    lhsT=wc[:, 128 * q : 128 * q + 128].bitcast(FP8X4),
-                    lhsT_scale=ws[:, 128 * q : 128 * q + 128],
+                    out=yt[:, b, :],
+                    lhsT=wc[:, 128 * b : 128 * b + 128].bitcast(FP8X4),
+                    lhsT_scale=ws[:, 128 * b : 128 * b + 128],
                     rhs=xc[:, cols].bitcast(FP8X4),
                     rhs_scale=xs[:, cols],
                     start=True,
@@ -218,7 +221,7 @@ def tile_fluxattention_pa_t_kernel(
                 return
             wc, ws = w_q[0 if u < 4 * TEXT_GROUPS else 1]
             xc, xs = xq_tiles[u // 2]
-            vs = vpsum.tile([P, 256 + 4 * SUM_COLS], F32, name="vs")
+            vs = vpsum.tile([P, 256 + 2 * SUM_COLS], F32, name="vs")
             vs_tiles[u] = vs
             for a in range(2):
                 cols = slice(256 * (u % 2) + 128 * a, 256 * (u % 2) + 128 * a + 128)
@@ -243,37 +246,51 @@ def tile_fluxattention_pa_t_kernel(
             nc.scalar.activation(
                 out=sq[:].rearrange("p q r -> p (q r)"), in_=yt_tiles[u][:].rearrange("p q r -> p (q r)"), func=ACT.Square
             )
-            for q in range(2):
+            for b in range(2):
                 nc.scalar.activation(
-                    out=zt[:, q, :], in_=yt_tiles[u][:, q, :], func=ACT.Copy, scale=gain_col[:, 2 * s + q : 2 * s + q + 1]
+                    out=zt[:, b, :], in_=yt_tiles[u][:, b, :], func=ACT.Copy, scale=gain_col[:, b, s : s + 1]
                 )
+
+        def stage_fold(u):
+            if not valid(u):
+                return
+            fold = zpool.tile([P, 256], F32, name="fold")
+            fold_tiles[u] = fold
+            nc.gpsimd.tensor_tensor(out=fold[:], in0=sq_tiles[u][:, 0, :], in1=sq_tiles[u][:, 1, :], op=ALU.add)
 
         def stage_back(u):
             if not valid(u):
                 return
             z = zpsum.tile([P, 2, 2, 128], F32, name="z")
             z_tiles[u] = z
+            for a in range(2):
+                for b in range(2):
+                    nc.tensor.transpose(
+                        z[:, a].rearrange("p q (h b i) -> p b (q h) i", h=2, b=2)[:, b],
+                        zt_tiles[u][:, b, 128 * a : 128 * a + 128],
+                        ident[:],
+                    )
+
+        def stage_sums(u):
+            if not valid(u):
+                return
             vs = vs_tiles[u]
             for a in range(2):
-                for q in range(2):
-                    nc.tensor.matmul(
-                        out=vs[:, 256 + SUM_COLS * (2 * a + q) : 256 + SUM_COLS * (2 * a + q + 1)],
-                        lhsT=sq_tiles[u][:, q, 128 * a : 128 * a + 128],
-                        rhs=head_ones[:],
-                        start=True,
-                        stop=True,
-                    )
-            for a in range(2):
-                for q in range(2):
-                    nc.tensor.transpose(z[:, a, q, :], zt_tiles[u][:, q, 128 * a : 128 * a + 128], ident[:])
+                nc.tensor.matmul(
+                    out=vs[:, 256 + SUM_COLS * a : 256 + SUM_COLS * (a + 1)],
+                    lhsT=fold_tiles[u][:, 128 * a : 128 * a + 128],
+                    rhs=group_ones[:],
+                    start=True,
+                    stop=True,
+                )
 
         def stage_rstd_v(u):
             if not valid(u):
                 return
             rstd = stat.tile([P, 8], F32, name="rstd")
             nc.scalar.activation(
-                out=rstd[:].rearrange("p (j h) -> p j h", h=2),
-                in_=vs_tiles[u][:, 256 : 256 + 4 * SUM_COLS].rearrange("p (j n) -> p j n", n=SUM_COLS)[:, :, 0:2],
+                out=rstd[:].rearrange("p (a g) -> p a g", g=4),
+                in_=vs_tiles[u][:, 256 : 256 + 2 * SUM_COLS].rearrange("p (a n) -> p a n", n=SUM_COLS)[:, :, 0:4],
                 func=ACT.Abs_reciprocal_sqrt,
                 scale=1.0 / 64.0,
                 bias=EPS,
@@ -334,30 +351,36 @@ def tile_fluxattention_pa_t_kernel(
         w_q = {}
         w_q[0] = quantise_w(regroup_w(w_raw[0], "we", nc.vector.tensor_copy), "we")
         w_grouped_i = regroup_w(w_raw[1], "wi", nc.gpsimd.tensor_copy)
-        gain_col = const.tile([P, 4], F32, name="gain_col")
+        gain_col = const.tile([P, 2, 2], F32, name="gain_col")
 
         def gain_columns():
-            gain_perm = const.tile([P, 128], BF16, name="gain_perm")
-            nc.vector.tensor_copy(
-                out=gain_perm[:].rearrange("p (h b i) -> p h b i", h=2, b=2),
-                in_=gain_rows[:].rearrange("p (i b) -> p b i", b=2).unsqueeze(1).to_broadcast([P, 2, 2, 32]),
-            )
-            gain_ps = vpsum.tile([P, 128], BF16, name="vs")
-            nc.tensor.transpose(gain_ps[:], gain_perm[:], ident_bf[:])
-            nc.vector.tensor_copy(out=gain_col[:], in_=gain_ps[:, 0:4])
+            gain_perm = const.tile([P, 2, 128], BF16, name="gain_perm")
+            gain_ps = vpsum.tile([P, 2, 128], BF16, name="vs")
+            for b in range(2):
+                nc.vector.tensor_copy(
+                    out=gain_perm[:, b, :].rearrange("p (q h i) -> p q h i", q=2, h=2),
+                    in_=gain_rows[:]
+                    .rearrange("p (q i b) -> p b q i", q=2, b=2)[:, b]
+                    .unsqueeze(2)
+                    .to_broadcast([P, 2, 2, 32]),
+                )
+                nc.tensor.transpose(gain_ps[:, b, :], gain_perm[:, b, :], ident_bf[:])
+            nc.vector.tensor_copy(out=gain_col[:], in_=gain_ps[:, :, 0:2])
 
         for i in range(-6, N_UNITS + 2):
+            stage_rstd_v(i - 1)
             stage_back(i)
             stage_transpose(i + 6)
+            stage_sums(i)
             stage_gain_square(i + 1)
-            stage_products(i - 1)
+            stage_add(i - 2)
+            stage_fold(i + 1)
             stage_copy(i + 5)
-            stage_rstd_v(i)
             if i % 2 == 1:
                 stage_quantise((i + 3) // 2)
+            stage_products(i - 1)
             stage_matmul_qk(i + 2)
             stage_matmul_v(i + 1)
-            stage_add(i - 2)
             if i == -5:
                 gain_columns()
             if i == 1:

@@ -21,7 +21,7 @@ TEXT_GROUPS = 2
 N_UNITS = 32
 CHUNK_TILES = 4
 N_CHUNKS = 16
-SUM_COLS = 128
+SUM_COLS = 64
 
 
 def tile_fluxattention_pa_t_kernel(
@@ -251,8 +251,11 @@ def tile_fluxattention_pa_t_kernel(
                     out=zt[:, b, :], in_=yt_tiles[u][:, b, :], func=ACT.Copy, scale=gain_col[:, b, s : s + 1]
                 )
 
+        def folded(u):
+            return u % 2 == 1
+
         def stage_fold(u):
-            if not valid(u):
+            if not valid(u) or not folded(u):
                 return
             fold = zpool.tile([P, 256], F32, name="fold")
             fold_tiles[u] = fold
@@ -276,13 +279,18 @@ def tile_fluxattention_pa_t_kernel(
                 return
             vs = vs_tiles[u]
             for a in range(2):
-                nc.tensor.matmul(
-                    out=vs[:, 256 + SUM_COLS * a : 256 + SUM_COLS * (a + 1)],
-                    lhsT=fold_tiles[u][:, 128 * a : 128 * a + 128],
-                    rhs=group_ones[:],
-                    start=True,
-                    stop=True,
-                )
+                if folded(u):
+                    parts = [fold_tiles[u][:, 128 * a : 128 * a + 128]]
+                else:
+                    parts = [sq_tiles[u][:, b, 128 * a : 128 * a + 128] for b in range(2)]
+                for k, part in enumerate(parts):
+                    nc.tensor.matmul(
+                        out=vs[:, 256 + SUM_COLS * a : 256 + SUM_COLS * (a + 1)],
+                        lhsT=part,
+                        rhs=group_ones[:],
+                        start=(k == 0),
+                        stop=(k == len(parts) - 1),
+                    )
 
         def stage_rstd_v(u):
             if not valid(u):

@@ -52,7 +52,7 @@ def tile_fluxattention_pa_t_kernel(
         fpool = ctx.enter_context(tc.tile_pool(name="fpool", bufs=N_GROUPS))
         gpool = ctx.enter_context(tc.tile_pool(name="gpool", bufs=3))
         cpool = ctx.enter_context(tc.tile_pool(name="cpool", bufs=4))
-        zpool = ctx.enter_context(tc.tile_pool(name="zpool", bufs=3))
+        zpool = ctx.enter_context(tc.tile_pool(name="zpool", bufs=4))
         ppool = ctx.enter_context(tc.tile_pool(name="ppool", bufs=3))
         opool = ctx.enter_context(tc.tile_pool(name="opool", bufs=4))
         stat = ctx.enter_context(tc.tile_pool(name="stat", bufs=4))
@@ -221,8 +221,7 @@ def tile_fluxattention_pa_t_kernel(
                 return
             wc, ws = w_q[0 if u < 4 * TEXT_GROUPS else 1]
             xc, xs = xq_tiles[u // 2]
-            vs = vpsum.tile([P, 256 + 2 * SUM_COLS], F32, name="vs")
-            vs_tiles[u] = vs
+            vs = vs_tiles[u]
             for a in range(2):
                 cols = slice(256 * (u % 2) + 128 * a, 256 * (u % 2) + 128 * a + 128)
                 nc.tensor.matmul_mx(
@@ -277,7 +276,8 @@ def tile_fluxattention_pa_t_kernel(
         def stage_sums(u):
             if not valid(u):
                 return
-            vs = vs_tiles[u]
+            vs = vpsum.tile([P, 256 + 2 * SUM_COLS], F32, name="vs")
+            vs_tiles[u] = vs
             for a in range(2):
                 if folded(u):
                     parts = [fold_tiles[u][:, 128 * a : 128 * a + 128]]
@@ -375,21 +375,21 @@ def tile_fluxattention_pa_t_kernel(
                 nc.tensor.transpose(gain_ps[:, b, :], gain_perm[:, b, :], ident_bf[:])
             nc.vector.tensor_copy(out=gain_col[:], in_=gain_ps[:, :, 0:2])
 
-        for i in range(-6, N_UNITS + 2):
-            stage_rstd_v(i - 1)
-            stage_back(i)
-            stage_transpose(i + 6)
-            stage_sums(i)
-            stage_gain_square(i + 1)
+        for i in range(-7, N_UNITS + 2):
+            stage_rstd_v(i)
+            stage_sums(i + 1)
+            stage_gain_square(i + 2)
             stage_add(i - 2)
-            stage_fold(i + 1)
-            stage_copy(i + 5)
-            if i % 2 == 1:
-                stage_quantise((i + 3) // 2)
+            stage_fold(i + 2)
             stage_products(i - 1)
-            stage_matmul_qk(i + 2)
+            stage_copy(i + 6)
+            if i % 2 == 0:
+                stage_quantise((i + 4) // 2)
+            stage_matmul_qk(i + 3)
             stage_matmul_v(i + 1)
-            if i == -5:
+            stage_back(i)
+            stage_transpose(i + 7)
+            if i == -6:
                 gain_columns()
             if i == 1:
                 w_q[1] = quantise_w(w_grouped_i, "wi")

@@ -72,17 +72,16 @@ def tile_fluxattention_pa_t_kernel(
             nc.sync.dma_start(out=raw[:], in_=w.rearrange("(p t) c -> p t c", t=4))
             return raw
 
-        def load_x(c, pieces):
+        def load_x_part(xt, c, lo, hi):
             if c < 2 * TEXT_GROUPS:
                 src, cc = x_txt, c
             else:
                 src, cc = x_img, c - 2 * TEXT_GROUPS
+            nc.sync.dma_start(out=xt[:, lo:hi, :], in_=chunk_rows(src, cc, lo, hi))
+
+        def load_x(c):
             xt = xpool.tile([P, CHUNK_TILES, 512], BF16, name="x")
-            step = CHUNK_TILES // pieces
-            for k in range(pieces):
-                nc.sync.dma_start(
-                    out=xt[:, step * k : step * k + step, :], in_=chunk_rows(src, cc, step * k, step * k + step)
-                )
+            load_x_part(xt, c, 0, CHUNK_TILES)
             return xt
 
         def load_f(grp):
@@ -99,18 +98,21 @@ def tile_fluxattention_pa_t_kernel(
         x_tiles = {}
         f_tiles = {}
         w_raw = {}
+        x_first = xpool.tile([P, CHUNK_TILES, 512], BF16, name="x")
+        x_tiles[0] = x_first
+        load_x_part(x_first, 0, 0, 2)
         w_raw[0] = load_w(W_eqkv, "we")
-        x_tiles[0] = load_x(0, 2)
+        load_x_part(x_first, 0, 2, 4)
         for j, g in enumerate((eqn_scale, ekn_scale, qn_scale, kn_scale)):
             nc.sync.dma_start(
                 out=gain_rows[j // 2 : j // 2 + 1, 64 * (j % 2) : 64 * (j % 2) + 64], in_=g.rearrange("(o d) -> o d", o=1)
             )
-        x_tiles[1] = load_x(1, 1)
+        x_tiles[1] = load_x(1)
         f_tiles[0] = load_f(0)
         w_raw[1] = load_w(W_iqkv, "wi")
         f_tiles[1] = load_f(1)
         for c in range(2, N_CHUNKS):
-            x_tiles[c] = load_x(c, 1)
+            x_tiles[c] = load_x(c)
             if c < N_GROUPS:
                 f_tiles[c] = load_f(c)
 
@@ -346,15 +348,19 @@ def tile_fluxattention_pa_t_kernel(
                 o_tiles[c] = o_new
             lo = 2 * (u % 2)
             pv = prod_tiles[c][:, :, lo : lo + 2].rearrange("p q t h (b c) -> p q (t h) b c", b=2)
-            nc.gpsimd.tensor_tensor(
+            engine = nc.vector if u == N_UNITS - 1 else nc.gpsimd
+            engine.tensor_tensor(
                 out=o_tiles[c][:, :, lo : lo + 2, :].rearrange("p q t (h c) -> p q (t h) c", h=2),
                 in0=pv[:, :, :, 0, :],
                 in1=pv[:, :, :, 1, :],
                 op=ALU.add,
             )
-            if u % 2 == 1:
-                nc.sync.dma_start(out=chunk_rows(outs[0], c, 0, CHUNK_TILES), in_=o_tiles[c][:, 0])
-                nc.sync.dma_start(out=chunk_rows(outs[1], c, 0, CHUNK_TILES), in_=o_tiles[c][:, 1])
+            if c == N_CHUNKS - 1:
+                for q in range(2):
+                    nc.sync.dma_start(out=chunk_rows(outs[q], c, lo, lo + 2), in_=o_tiles[c][:, q, lo : lo + 2, :])
+            elif u % 2 == 1:
+                for q in range(2):
+                    nc.sync.dma_start(out=chunk_rows(outs[q], c, 0, CHUNK_TILES), in_=o_tiles[c][:, q])
 
         w_q = {}
         w_q[0] = quantise_w(regroup_w(w_raw[0], "we", nc.vector.tensor_copy), "we")
@@ -375,13 +381,16 @@ def tile_fluxattention_pa_t_kernel(
                 nc.tensor.transpose(gain_ps[:, b, :], gain_perm[:, b, :], ident_bf[:])
             nc.vector.tensor_copy(out=gain_col[:], in_=gain_ps[:, :, 0:2])
 
-        for i in range(-7, N_UNITS + 2):
+        for i in range(-7, N_UNITS + 1):
             stage_rstd_v(i)
             stage_sums(i + 1)
             stage_gain_square(i + 2)
-            stage_add(i - 2)
+            if i - 2 < N_UNITS - 1:
+                stage_add(i - 2)
             stage_fold(i + 2)
             stage_products(i - 1)
+            if i - 1 == N_UNITS - 1:
+                stage_add(i - 1)
             stage_copy(i + 6)
             if i % 2 == 0:
                 stage_quantise((i + 4) // 2)

@@ -52,7 +52,7 @@ def tile_fluxattention_pa_t_kernel(
         fpool = ctx.enter_context(tc.tile_pool(name="fpool", bufs=N_GROUPS))
         gpool = ctx.enter_context(tc.tile_pool(name="gpool", bufs=3))
         cpool = ctx.enter_context(tc.tile_pool(name="cpool", bufs=4))
-        zpool = ctx.enter_context(tc.tile_pool(name="zpool", bufs=4))
+        zpool = ctx.enter_context(tc.tile_pool(name="zpool", bufs=5))
         ppool = ctx.enter_context(tc.tile_pool(name="ppool", bufs=3))
         opool = ctx.enter_context(tc.tile_pool(name="opool", bufs=4))
         stat = ctx.enter_context(tc.tile_pool(name="stat", bufs=4))
@@ -381,24 +381,24 @@ def tile_fluxattention_pa_t_kernel(
                 nc.tensor.transpose(gain_ps[:, b, :], gain_perm[:, b, :], ident_bf[:])
             nc.vector.tensor_copy(out=gain_col[:], in_=gain_ps[:, :, 0:2])
 
-        for i in range(-7, N_UNITS + 1):
+        for i in range(-8, N_UNITS + 1):
             stage_rstd_v(i)
             stage_sums(i + 1)
-            stage_gain_square(i + 2)
+            stage_gain_square(i + 3)
+            stage_fold(i + 2)
             if i - 2 < N_UNITS - 1:
                 stage_add(i - 2)
-            stage_fold(i + 2)
             stage_products(i - 1)
             if i - 1 == N_UNITS - 1:
                 stage_add(i - 1)
-            stage_copy(i + 6)
-            if i % 2 == 0:
-                stage_quantise((i + 4) // 2)
-            stage_matmul_qk(i + 3)
+            stage_copy(i + 7)
+            if i % 2 == 1:
+                stage_quantise((i + 5) // 2)
+            stage_matmul_qk(i + 4)
             stage_matmul_v(i + 1)
             stage_back(i)
-            stage_transpose(i + 7)
-            if i == -6:
+            stage_transpose(i + 8)
+            if i == -7:
                 gain_columns()
             if i == 1:
                 w_q[1] = quantise_w(w_grouped_i, "wi")

@@ -128,6 +128,9 @@ def tile_fluxattention_pa_t_kernel(
         for g in range(4):
             nc.vector.memset(group_ones[32 * g : 32 * g + 32, g : g + 1], 1.0)
 
+        def gpsimd_copy(out, in_):
+            nc.gpsimd.tensor_scalar(out=out, in0=in_, scalar1=1.0, scalar2=0.0, op0=ALU.mult, op1=ALU.add)
+
         def regroup_w(raw, name, copy):
             grouped = const.tile([P, 384, 4], BF16, name=name + "_grouped", align_bytes=64)
             for b in range(2):
@@ -364,7 +367,7 @@ def tile_fluxattention_pa_t_kernel(
 
         w_q = {}
         w_q[0] = quantise_w(regroup_w(w_raw[0], "we", nc.vector.tensor_copy), "we")
-        w_grouped_i = regroup_w(w_raw[1], "wi", nc.gpsimd.tensor_copy)
+        w_grouped_i = regroup_w(w_raw[1], "wi", gpsimd_copy)
         gain_col = const.tile([P, 2, 2], F32, name="gain_col")
 
         def gain_columns():

@@ -92,6 +92,9 @@ def tile_fluxattention_pa_t_kernel(
             )
             return ft
 
+        zeros = const.tile([P, 256], F32, name="zeros")
+        nc.vector.memset(zeros[:], 0.0)
+
         gain_rows = const.tile([P, 128], BF16, name="gain_rows")
         nc.vector.memset(gain_rows[:], 0.0)
 
@@ -101,12 +104,12 @@ def tile_fluxattention_pa_t_kernel(
         x_first = xpool.tile([P, CHUNK_TILES, 512], BF16, name="x")
         x_tiles[0] = x_first
         load_x_part(x_first, 0, 0, 2)
-        w_raw[0] = load_w(W_eqkv, "we")
-        load_x_part(x_first, 0, 2, 4)
         for j, g in enumerate((eqn_scale, ekn_scale, qn_scale, kn_scale)):
             nc.sync.dma_start(
                 out=gain_rows[j // 2 : j // 2 + 1, 64 * (j % 2) : 64 * (j % 2) + 64], in_=g.rearrange("(o d) -> o d", o=1)
             )
+        w_raw[0] = load_w(W_eqkv, "we")
+        load_x_part(x_first, 0, 2, 4)
         x_tiles[1] = load_x(1)
         f_tiles[0] = load_f(0)
         w_raw[1] = load_w(W_iqkv, "wi")
@@ -168,6 +171,16 @@ def tile_fluxattention_pa_t_kernel(
 
         def valid(u):
             return 0 <= u < N_UNITS
+
+        def keep_clock(n):
+            idle = zpsum.tile([P, 2, 2, 128], F32, name="z")
+            nc.tensor.matmul(
+                out=idle[:].rearrange("p a q c -> p (a q c)")[:, 0:n],
+                lhsT=zeros[:, 0:128],
+                rhs=zeros[:, 0:n],
+                start=True,
+                stop=True,
+            )
 
         def stage_transpose(u):
             if not valid(u):
@@ -290,9 +303,9 @@ def tile_fluxattention_pa_t_kernel(
                     parts = [sq_tiles[u][:, b, 128 * a : 128 * a + 128] for b in range(2)]
                 for k, part in enumerate(parts):
                     nc.tensor.matmul(
-                        out=vs[:, 256 + SUM_COLS * a : 256 + SUM_COLS * (a + 1)],
+                        out=vs[:, 256 + SUM_COLS * a : 256 + SUM_COLS * a + SUM_COLS // len(parts)],
                         lhsT=part,
-                        rhs=group_ones[:],
+                        rhs=group_ones[:, 0 : SUM_COLS // len(parts)],
                         start=(k == 0),
                         stop=(k == len(parts) - 1),
                     )
@@ -365,22 +378,25 @@ def tile_fluxattention_pa_t_kernel(
                 for q in range(2):
                     nc.sync.dma_start(out=chunk_rows(outs[q], c, 0, CHUNK_TILES), in_=o_tiles[c][:, q])
 
+        gain_perm = const.tile([P, 2, 128], BF16, name="gain_perm")
+        for b in range(2):
+            nc.vector.tensor_copy(
+                out=gain_perm[:, b, :].rearrange("p (q h i) -> p q h i", q=2, h=2),
+                in_=gain_rows[:]
+                .rearrange("p (q i b) -> p b q i", q=2, b=2)[:, b]
+                .unsqueeze(2)
+                .to_broadcast([P, 2, 2, 32]),
+            )
+        for n in (256, 256):
+            keep_clock(n)
         w_q = {}
         w_q[0] = quantise_w(regroup_w(w_raw[0], "we", nc.vector.tensor_copy), "we")
         w_grouped_i = regroup_w(w_raw[1], "wi", gpsimd_copy)
         gain_col = const.tile([P, 2, 2], F32, name="gain_col")
 
         def gain_columns():
-            gain_perm = const.tile([P, 2, 128], BF16, name="gain_perm")
             gain_ps = vpsum.tile([P, 2, 128], BF16, name="vs")
             for b in range(2):
-                nc.vector.tensor_copy(
-                    out=gain_perm[:, b, :].rearrange("p (q h i) -> p q h i", q=2, h=2),
-                    in_=gain_rows[:]
-                    .rearrange("p (q i b) -> p b q i", q=2, b=2)[:, b]
-                    .unsqueeze(2)
-                    .to_broadcast([P, 2, 2, 32]),
-                )
                 nc.tensor.transpose(gain_ps[:, b, :], gain_perm[:, b, :], ident_bf[:])
             nc.vector.tensor_copy(out=gain_col[:], in_=gain_ps[:, :, 0:2])
 
@@ -401,6 +417,8 @@ def tile_fluxattention_pa_t_kernel(
             stage_matmul_v(i + 1)
             stage_back(i)
             stage_transpose(i + 8)
+            if i < 2:
+                keep_clock(256 if i < -4 else 128)
             if i == -7:
                 gain_columns()
             if i == 1:

@@ -50,9 +50,9 @@ def tile_fluxattention_pa_t_kernel(
         const = ctx.enter_context(tc.tile_pool(name="const", bufs=1))
         xpool = ctx.enter_context(tc.tile_pool(name="xpool", bufs=N_CHUNKS))
         fpool = ctx.enter_context(tc.tile_pool(name="fpool", bufs=N_GROUPS))
-        gpool = ctx.enter_context(tc.tile_pool(name="gpool", bufs=3))
-        cpool = ctx.enter_context(tc.tile_pool(name="cpool", bufs=4))
-        zpool = ctx.enter_context(tc.tile_pool(name="zpool", bufs=5))
+        gpool = ctx.enter_context(tc.tile_pool(name="gpool", bufs=4))
+        cpool = ctx.enter_context(tc.tile_pool(name="cpool", bufs=9))
+        zpool = ctx.enter_context(tc.tile_pool(name="zpool", bufs=6))
         ppool = ctx.enter_context(tc.tile_pool(name="ppool", bufs=3))
         opool = ctx.enter_context(tc.tile_pool(name="opool", bufs=4))
         stat = ctx.enter_context(tc.tile_pool(name="stat", bufs=4))
@@ -98,26 +98,45 @@ def tile_fluxattention_pa_t_kernel(
         gain_rows = const.tile([P, 128], BF16, name="gain_rows")
         nc.vector.memset(gain_rows[:], 0.0)
 
+        def load_gains():
+            for j, g in enumerate((eqn_scale, ekn_scale, qn_scale, kn_scale)):
+                nc.sync.dma_start(
+                    out=gain_rows[j // 2 : j // 2 + 1, 64 * (j % 2) : 64 * (j % 2) + 64], in_=g.rearrange("(o d) -> o d", o=1)
+                )
+
         x_tiles = {}
         f_tiles = {}
         w_raw = {}
         x_first = xpool.tile([P, CHUNK_TILES, 512], BF16, name="x")
         x_tiles[0] = x_first
         load_x_part(x_first, 0, 0, 2)
-        for j, g in enumerate((eqn_scale, ekn_scale, qn_scale, kn_scale)):
-            nc.sync.dma_start(
-                out=gain_rows[j // 2 : j // 2 + 1, 64 * (j % 2) : 64 * (j % 2) + 64], in_=g.rearrange("(o d) -> o d", o=1)
-            )
+        load_gains()
         w_raw[0] = load_w(W_eqkv, "we")
         load_x_part(x_first, 0, 2, 4)
         x_tiles[1] = load_x(1)
         f_tiles[0] = load_f(0)
+        x_tiles[2] = load_x(2)
+        x_tiles[3] = load_x(3)
         w_raw[1] = load_w(W_iqkv, "wi")
         f_tiles[1] = load_f(1)
-        for c in range(2, N_CHUNKS):
-            x_tiles[c] = load_x(c)
-            if c < N_GROUPS:
-                f_tiles[c] = load_f(c)
+        x_tiles[4] = load_x(4)
+        f_tiles[2] = load_f(2)
+        x_tiles[5] = load_x(5)
+        x_tiles[6] = load_x(6)
+        f_tiles[3] = load_f(3)
+        x_tiles[7] = load_x(7)
+        x_tiles[8] = load_x(8)
+        f_tiles[4] = load_f(4)
+        x_tiles[9] = load_x(9)
+        x_tiles[10] = load_x(10)
+        f_tiles[5] = load_f(5)
+        x_tiles[11] = load_x(11)
+        x_tiles[12] = load_x(12)
+        f_tiles[6] = load_f(6)
+        x_tiles[13] = load_x(13)
+        x_tiles[14] = load_x(14)
+        f_tiles[7] = load_f(7)
+        x_tiles[15] = load_x(15)
 
         ident = const.tile([P, P], F32, name="ident")
         make_identity(nc, ident[:])
@@ -131,29 +150,35 @@ def tile_fluxattention_pa_t_kernel(
         for g in range(4):
             nc.vector.memset(group_ones[32 * g : 32 * g + 32, g : g + 1], 1.0)
 
-        def gpsimd_copy(out, in_):
-            nc.gpsimd.tensor_scalar(out=out, in0=in_, scalar1=1.0, scalar2=0.0, op0=ALU.mult, op1=ALU.add)
+        wg = {}
+        w_q = {}
 
-        def regroup_w(raw, name, copy):
-            grouped = const.tile([P, 384, 4], BF16, name=name + "_grouped", align_bytes=64)
-            for b in range(2):
+        def regroup_w(s, part, copy):
+            name, raw = ("we", "wi")[s], w_raw[s]
+            if s not in wg:
+                grouped = const.tile([P, 384, 4], BF16, name=name + "_grouped", align_bytes=64)
+                codes = const.tile([P, 384], U32, name=name + "_codes", align_bytes=64)
+                scales = const.tile([P, 384], U8, name=name + "_scales", align_bytes=64)
+                wg[s] = grouped
+                w_q[s] = (codes, scales)
+            grouped = wg[s]
+            if part < 2:
+                b = part
                 copy(
                     out=grouped[:, 128 * b : 128 * b + 128, :],
                     in_=raw[:, :, 0:256].rearrange("p t (c b) -> p b c t", b=2)[:, b],
                 )
-            copy(out=grouped[:, 256:384, :], in_=raw[:, :, 256:384].rearrange("p t n -> p n t"))
-            return grouped
+            else:
+                copy(out=grouped[:, 256:384, :], in_=raw[:, :, 256:384].rearrange("p t n -> p n t"))
 
-        def quantise_w(grouped, name):
-            codes = const.tile([P, 384], U32, name=name + "_codes", align_bytes=64)
-            scales = const.tile([P, 384], U8, name=name + "_scales", align_bytes=64)
-            for lo, hi in ((0, 256), (256, 384)):
-                nc.vector.quantize_mx(
-                    out=codes[:, lo:hi].bitcast(FP8X4),
-                    scales=scales[:, lo:hi],
-                    in_=grouped[:, lo:hi, :].rearrange("p n t -> p (n t)"),
-                )
-            return codes, scales
+        def quantise_w(s, part):
+            codes, scales = w_q[s]
+            lo, hi = ((0, 256), (256, 384))[part]
+            nc.vector.quantize_mx(
+                out=codes[:, lo:hi].bitcast(FP8X4),
+                scales=scales[:, lo:hi],
+                in_=wg[s][:, lo:hi, :].rearrange("p n t -> p (n t)"),
+            )
 
         xt_tiles = {}
         xg_tiles = {}
@@ -169,9 +194,6 @@ def tile_fluxattention_pa_t_kernel(
         o_tiles = {}
         vsb_tiles = {}
 
-        def valid(u):
-            return 0 <= u < N_UNITS
-
         def keep_clock(n):
             idle = zpsum.tile([P, 2, 2, 128], F32, name="z")
             nc.tensor.matmul(
@@ -183,23 +205,21 @@ def tile_fluxattention_pa_t_kernel(
             )
 
         def stage_transpose(u):
-            if not valid(u):
-                return
             xw = x_tiles[u // 2][:].bitcast(F32)
             xt = tpsum.tile([P, 2, 2, 128], F32, name="xt")
             xt_tiles[u] = xt
             for a in range(2):
                 for half in range(2):
                     nc.tensor.transpose(xt[:, a, half, :], xw[:, 2 * (u % 2) + a, half : 256 : 2], ident[:])
+            if u < 3:
+                keep_clock(256 if u < 2 else 128)
 
         def stage_copy(u):
-            if not valid(u):
-                return
             if u % 2 == 0:
                 xg_new = gpool.tile([P, 2048], BF16, name="xg", align_bytes=64)
                 xg_tiles[u // 2] = xg_new
             xg = xg_tiles[u // 2]
-            copy = nc.scalar.copy if u % 2 == 0 else nc.vector.tensor_copy
+            copy = nc.scalar.copy if ("SSVVVV"[u] if u < 6 else "SVSV"[u % 4]) == "S" else nc.vector.tensor_copy
             copy(
                 out=xg[:, 1024 * (u % 2) : 1024 * (u % 2) + 1024]
                 .bitcast(F32)
@@ -207,17 +227,20 @@ def tile_fluxattention_pa_t_kernel(
                 in_=xt_tiles[u][:].rearrange("p a h r -> p a r h"),
             )
 
-        def stage_quantise(c):
-            if not 0 <= c < N_CHUNKS:
-                return
-            xc = cpool.tile([P, 512], U32, name="xc", align_bytes=64)
-            xs = cpool.tile([P, 512], U8, name="xs", align_bytes=64)
-            nc.vector.quantize_mx(out=xc[:].bitcast(FP8X4), scales=xs[:], in_=xg_tiles[c][:])
-            xq_tiles[c] = (xc, xs)
+        def stage_quantise(u):
+            c = u // 2
+            split = False
+            if u % 2 == 0:
+                xc_new = cpool.tile([P, 512], U32, name="xc", align_bytes=64)
+                xs_new = cpool.tile([P, 512], U8, name="xs", align_bytes=64)
+                xq_tiles[c] = (xc_new, xs_new)
+                if not split:
+                    return
+            xc, xs = xq_tiles[c]
+            lo, hi = ((0, 256) if u % 2 == 0 else (256, 512)) if split else (0, 512)
+            nc.vector.quantize_mx(out=xc[:, lo:hi].bitcast(FP8X4), scales=xs[:, lo:hi], in_=xg_tiles[c][:, 4 * lo : 4 * hi])
 
         def stage_matmul_qk(u):
-            if not valid(u):
-                return
             wc, ws = w_q[0 if u < 4 * TEXT_GROUPS else 1]
             xc, xs = xq_tiles[u // 2]
             yt = ypsum.tile([P, 2, 256], F32, name="yt")
@@ -235,8 +258,6 @@ def tile_fluxattention_pa_t_kernel(
                 )
 
         def stage_matmul_v(u):
-            if not valid(u):
-                return
             wc, ws = w_q[0 if u < 4 * TEXT_GROUPS else 1]
             xc, xs = xq_tiles[u // 2]
             vs = vs_tiles[u]
@@ -253,8 +274,6 @@ def tile_fluxattention_pa_t_kernel(
                 )
 
         def stage_gain_square(u):
-            if not valid(u):
-                return
             s = 0 if u < 4 * TEXT_GROUPS else 1
             zt = zpool.tile([P, 2, 256], F32, name="zt")
             zt_tiles[u] = zt
@@ -269,18 +288,17 @@ def tile_fluxattention_pa_t_kernel(
                 )
 
         def folded(u):
-            return u % 2 == 1
+            return int("1211"[u % 4]) if u >= 3 else 0
 
         def stage_fold(u):
-            if not valid(u) or not folded(u):
+            if not folded(u):
                 return
             fold = zpool.tile([P, 256], F32, name="fold")
             fold_tiles[u] = fold
-            nc.gpsimd.tensor_tensor(out=fold[:], in0=sq_tiles[u][:, 0, :], in1=sq_tiles[u][:, 1, :], op=ALU.add)
+            w = 128 * folded(u)
+            nc.gpsimd.tensor_tensor(out=fold[:, 0:w], in0=sq_tiles[u][:, 0, 0:w], in1=sq_tiles[u][:, 1, 0:w], op=ALU.add)
 
         def stage_back(u):
-            if not valid(u):
-                return
             z = zpsum.tile([P, 2, 2, 128], F32, name="z")
             z_tiles[u] = z
             for a in range(2):
@@ -292,27 +310,23 @@ def tile_fluxattention_pa_t_kernel(
                     )
 
         def stage_sums(u):
-            if not valid(u):
-                return
             vs = vpsum.tile([P, 256 + 2 * SUM_COLS], F32, name="vs")
             vs_tiles[u] = vs
             for a in range(2):
-                if folded(u):
+                if a < folded(u):
                     parts = [fold_tiles[u][:, 128 * a : 128 * a + 128]]
                 else:
                     parts = [sq_tiles[u][:, b, 128 * a : 128 * a + 128] for b in range(2)]
                 for k, part in enumerate(parts):
                     nc.tensor.matmul(
-                        out=vs[:, 256 + SUM_COLS * a : 256 + SUM_COLS * a + SUM_COLS // len(parts)],
+                        out=vs[:, 256 + SUM_COLS * a : 256 + SUM_COLS * (a + 1)],
                         lhsT=part,
-                        rhs=group_ones[:, 0 : SUM_COLS // len(parts)],
+                        rhs=group_ones[:],
                         start=(k == 0),
                         stop=(k == len(parts) - 1),
                     )
 
         def stage_rstd_v(u):
-            if not valid(u):
-                return
             rstd = stat.tile([P, 8], F32, name="rstd")
             nc.scalar.activation(
                 out=rstd[:].rearrange("p (a g) -> p a g", g=4),
@@ -333,8 +347,6 @@ def tile_fluxattention_pa_t_kernel(
                 nc.sync.dma_start(out=chunk_rows(outs[2], u // 2, 0, CHUNK_TILES), in_=vsb[:])
 
         def stage_products(u):
-            if not valid(u):
-                return
             grp, t0 = divmod(2 * u, GROUP_TILES)
             if u % 2 == 0:
                 prod_new = ppool.tile([P, 2, CHUNK_TILES, 2, 128], F32, name="prod")
@@ -356,8 +368,6 @@ def tile_fluxattention_pa_t_kernel(
                     )
 
         def stage_add(u):
-            if not valid(u):
-                return
             c = u // 2
             if u % 2 == 0:
                 o_new = opool.tile([P, 2, CHUNK_TILES, 128], F32, name="o")
@@ -387,11 +397,6 @@ def tile_fluxattention_pa_t_kernel(
                 .unsqueeze(2)
                 .to_broadcast([P, 2, 2, 32]),
             )
-        for n in (256, 256):
-            keep_clock(n)
-        w_q = {}
-        w_q[0] = quantise_w(regroup_w(w_raw[0], "we", nc.vector.tensor_copy), "we")
-        w_grouped_i = regroup_w(w_raw[1], "wi", gpsimd_copy)
         gain_col = const.tile([P, 2, 2], F32, name="gain_col")
 
         def gain_columns():
@@ -400,26 +405,47 @@ def tile_fluxattention_pa_t_kernel(
                 nc.tensor.transpose(gain_ps[:, b, :], gain_perm[:, b, :], ident_bf[:])
             nc.vector.tensor_copy(out=gain_col[:], in_=gain_ps[:, :, 0:2])
 
-        for i in range(-8, N_UNITS + 1):
-            stage_rstd_v(i)
-            stage_sums(i + 1)
-            stage_gain_square(i + 3)
-            stage_fold(i + 2)
-            if i - 2 < N_UNITS - 1:
-                stage_add(i - 2)
-            stage_products(i - 1)
-            if i - 1 == N_UNITS - 1:
-                stage_add(i - 1)
-            stage_copy(i + 7)
-            if i % 2 == 1:
-                stage_quantise((i + 5) // 2)
-            stage_matmul_qk(i + 4)
-            stage_matmul_v(i + 1)
-            stage_back(i)
-            stage_transpose(i + 8)
-            if i < 2:
-                keep_clock(256 if i < -4 else 128)
-            if i == -7:
+        for k in range(3):
+            keep_clock(256)
+        for part in range(3):
+            regroup_w(0, part, nc.vector.tensor_copy)
+        quantise_w(0, 0)
+        quantise_w(0, 1)
+
+        issued = {}
+
+        def advance(stage, upto):
+            for u in range(issued.get(stage, 0), min(upto, N_UNITS - 1) + 1):
+                stage(u)
+                issued[stage] = u + 1
+
+        leads = (
+            (stage_rstd_v, 0, 0, 0),
+            (stage_back, 0, 0, 0),
+            (stage_sums, 1, 0, 1),
+            (stage_products, -1, 0, -1),
+            (stage_gain_square, 2, -1, 3),
+            (stage_quantise, 6, 0, 6),
+            (stage_add, -2, 0, -2),
+            (stage_matmul_v, 1, 0, 1),
+            (stage_matmul_qk, 4, -1, 4),
+            (stage_transpose, 8, 1, 8),
+            (stage_copy, 7, 0, 7),
+            (stage_fold, 3, -1, 2),
+        )
+        flags = set()
+        for step in range(-9, N_UNITS + 2):
+            for stage, first, ramp, lead in leads:
+                upto = step + (first if step < ramp else lead)
+                if stage == stage_quantise and upto % 2 == 0 and upto > -1:
+                    upto = upto - 1
+                advance(stage, upto)
+            if issued.get(stage_transpose, 0) >= 2 and "gains" not in flags:
+                flags.add("gains")
                 gain_columns()
-            if i == 1:
-                w_q[1] = quantise_w(w_grouped_i, "wi")
+            if step == -1:
+                for part in range(3):
+                    regroup_w(1, part, nc.gpsimd.tensor_copy)
+            if step == 0:
+                quantise_w(1, 0)
+                quantise_w(1, 1)

@@ -114,29 +114,29 @@ def tile_fluxattention_pa_t_kernel(
         w_raw[0] = load_w(W_eqkv, "we")
         load_x_part(x_first, 0, 2, 4)
         x_tiles[1] = load_x(1)
-        f_tiles[0] = load_f(0)
         x_tiles[2] = load_x(2)
+        f_tiles[0] = load_f(0)
         x_tiles[3] = load_x(3)
         w_raw[1] = load_w(W_iqkv, "wi")
-        f_tiles[1] = load_f(1)
         x_tiles[4] = load_x(4)
-        f_tiles[2] = load_f(2)
+        f_tiles[1] = load_f(1)
         x_tiles[5] = load_x(5)
-        x_tiles[6] = load_x(6)
         f_tiles[3] = load_f(3)
+        x_tiles[6] = load_x(6)
         x_tiles[7] = load_x(7)
-        x_tiles[8] = load_x(8)
         f_tiles[4] = load_f(4)
+        x_tiles[8] = load_x(8)
         x_tiles[9] = load_x(9)
-        x_tiles[10] = load_x(10)
         f_tiles[5] = load_f(5)
+        x_tiles[10] = load_x(10)
         x_tiles[11] = load_x(11)
-        x_tiles[12] = load_x(12)
         f_tiles[6] = load_f(6)
+        x_tiles[12] = load_x(12)
         x_tiles[13] = load_x(13)
-        x_tiles[14] = load_x(14)
         f_tiles[7] = load_f(7)
+        x_tiles[14] = load_x(14)
         x_tiles[15] = load_x(15)
+        f_tiles[2] = load_f(2)
 
         ident = const.tile([P, P], F32, name="ident")
         make_identity(nc, ident[:])
@@ -219,7 +219,7 @@ def tile_fluxattention_pa_t_kernel(
                 xg_new = gpool.tile([P, 2048], BF16, name="xg", align_bytes=64)
                 xg_tiles[u // 2] = xg_new
             xg = xg_tiles[u // 2]
-            copy = nc.scalar.copy if ("SSVVVV"[u] if u < 6 else "SVSV"[u % 4]) == "S" else nc.vector.tensor_copy
+            copy = nc.scalar.copy if ("SSVVVV"[u] if u < 6 else "SVSS"[u % 4]) == "S" else nc.vector.tensor_copy
             copy(
                 out=xg[:, 1024 * (u % 2) : 1024 * (u % 2) + 1024]
                 .bitcast(F32)
@@ -288,7 +288,7 @@ def tile_fluxattention_pa_t_kernel(
                 )
 
         def folded(u):
-            return int("1211"[u % 4]) if u >= 3 else 0
+            return int("2220"[u % 4]) if u >= 1 else 0
 
         def stage_fold(u):
             if not folded(u):
@@ -296,7 +296,7 @@ def tile_fluxattention_pa_t_kernel(
             fold = zpool.tile([P, 256], F32, name="fold")
             fold_tiles[u] = fold
             w = 128 * folded(u)
-            nc.gpsimd.tensor_tensor(out=fold[:, 0:w], in0=sq_tiles[u][:, 0, 0:w], in1=sq_tiles[u][:, 1, 0:w], op=ALU.add)
+            nc.vector.tensor_tensor(out=fold[:, 0:w], in0=sq_tiles[u][:, 0, 0:w], in1=sq_tiles[u][:, 1, 0:w], op=ALU.add)
 
         def stage_back(u):
             z = zpsum.tile([P, 2, 2, 128], F32, name="z")
@@ -411,6 +411,8 @@ def tile_fluxattention_pa_t_kernel(
             regroup_w(0, part, nc.vector.tensor_copy)
         quantise_w(0, 0)
         quantise_w(0, 1)
+        for part in range(3):
+            regroup_w(1, part, nc.gpsimd.tensor_copy)
 
         issued = {}
 
@@ -420,21 +422,21 @@ def tile_fluxattention_pa_t_kernel(
                 issued[stage] = u + 1
 
         leads = (
-            (stage_rstd_v, 0, 0, 0),
+            (stage_products, -1, 0, -1),
+            (stage_quantise, 6, 0, 6),
+            (stage_transpose, 7, 0, 7),
             (stage_back, 0, 0, 0),
             (stage_sums, 1, 0, 1),
-            (stage_products, -1, 0, -1),
-            (stage_gain_square, 2, -1, 3),
-            (stage_quantise, 6, 0, 6),
-            (stage_add, -2, 0, -2),
+            (stage_rstd_v, 0, 0, 0),
+            (stage_fold, 2, 0, 2),
             (stage_matmul_v, 1, 0, 1),
-            (stage_matmul_qk, 4, -1, 4),
-            (stage_transpose, 8, 1, 8),
+            (stage_add, -2, 0, -2),
             (stage_copy, 7, 0, 7),
-            (stage_fold, 3, -1, 2),
+            (stage_gain_square, 3, 0, 3),
+            (stage_matmul_qk, 4, 0, 4),
         )
         flags = set()
-        for step in range(-9, N_UNITS + 2):
+        for step in range(-8, N_UNITS + 2):
             for stage, first, ramp, lead in leads:
                 upto = step + (first if step < ramp else lead)
                 if stage == stage_quantise and upto % 2 == 0 and upto > -1:
@@ -443,9 +445,6 @@ def tile_fluxattention_pa_t_kernel(
             if issued.get(stage_transpose, 0) >= 2 and "gains" not in flags:
                 flags.add("gains")
                 gain_columns()
-            if step == -1:
-                for part in range(3):
-                    regroup_w(1, part, nc.gpsimd.tensor_copy)
-            if step == 0:
+            if step == 1:
                 quantise_w(1, 0)
                 quantise_w(1, 1)

@@ -288,7 +288,7 @@ def tile_fluxattention_pa_t_kernel(
                 )
 
         def folded(u):
-            return int("2220"[u % 4]) if u >= 1 else 0
+            return int("2222"[u % 4]) if u >= 1 else 0
 
         def stage_fold(u):
             if not folded(u):

@@ -54,7 +54,7 @@ def tile_fluxattention_pa_t_kernel(
         cpool = ctx.enter_context(tc.tile_pool(name="cpool", bufs=9))
         zpool = ctx.enter_context(tc.tile_pool(name="zpool", bufs=6))
         ppool = ctx.enter_context(tc.tile_pool(name="ppool", bufs=3))
-        opool = ctx.enter_context(tc.tile_pool(name="opool", bufs=4))
+        opool = ctx.enter_context(tc.tile_pool(name="opool", bufs=6))
         stat = ctx.enter_context(tc.tile_pool(name="stat", bufs=4))
         tpsum = ctx.enter_context(tc.psum_pool(name="tpsum", bufs=2))
         ypsum = ctx.enter_context(tc.psum_pool(name="ypsum", bufs=2))
@@ -219,7 +219,7 @@ def tile_fluxattention_pa_t_kernel(
                 xg_new = gpool.tile([P, 2048], BF16, name="xg", align_bytes=64)
                 xg_tiles[u // 2] = xg_new
             xg = xg_tiles[u // 2]
-            copy = nc.scalar.copy if ("SSVVVV"[u] if u < 6 else "SVSS"[u % 4]) == "S" else nc.vector.tensor_copy
+            copy = nc.scalar.copy if ("SSVVVV"[u] if u < 6 else "SSVSS"[u % 5]) == "S" else nc.vector.tensor_copy
             copy(
                 out=xg[:, 1024 * (u % 2) : 1024 * (u % 2) + 1024]
                 .bitcast(F32)
@@ -288,7 +288,7 @@ def tile_fluxattention_pa_t_kernel(
                 )
 
         def folded(u):
-            return int("2222"[u % 4]) if u >= 1 else 0
+            return int("2222220"[u % 7]) if 1 <= u < 30 else 0
 
         def stage_fold(u):
             if not folded(u):
@@ -424,16 +424,16 @@ def tile_fluxattention_pa_t_kernel(
         leads = (
             (stage_products, -1, 0, -1),
             (stage_quantise, 6, 0, 6),
+            (stage_fold, 2, 0, 2),
             (stage_transpose, 7, 0, 7),
             (stage_back, 0, 0, 0),
             (stage_sums, 1, 0, 1),
-            (stage_rstd_v, 0, 0, 0),
-            (stage_fold, 2, 0, 2),
             (stage_matmul_v, 1, 0, 1),
-            (stage_add, -2, 0, -2),
+            (stage_matmul_qk, 4, 0, 4),
+            (stage_rstd_v, 0, 0, 0),
             (stage_copy, 7, 0, 7),
             (stage_gain_square, 3, 0, 3),
-            (stage_matmul_qk, 4, 0, 4),
+            (stage_add, -2, 0, -2),
         )
         flags = set()
         for step in range(-8, N_UNITS + 2):

@@ -219,7 +219,7 @@ def tile_fluxattention_pa_t_kernel(
                 xg_new = gpool.tile([P, 2048], BF16, name="xg", align_bytes=64)
                 xg_tiles[u // 2] = xg_new
             xg = xg_tiles[u // 2]
-            copy = nc.scalar.copy if ("SSVVVV"[u] if u < 6 else "SSVSS"[u % 5]) == "S" else nc.vector.tensor_copy
+            copy = nc.scalar.copy if ("SSVVVVS"[u] if u < 7 else "SSSSV"[u % 5]) == "S" else nc.vector.tensor_copy
             copy(
                 out=xg[:, 1024 * (u % 2) : 1024 * (u % 2) + 1024]
                 .bitcast(F32)
@@ -288,7 +288,7 @@ def tile_fluxattention_pa_t_kernel(
                 )
 
         def folded(u):
-            return int("2222220"[u % 7]) if 1 <= u < 30 else 0
+            return int("0222222"[u % 7]) if 1 <= u < 31 else 0
 
         def stage_fold(u):
             if not folded(u):
@@ -422,18 +422,18 @@ def tile_fluxattention_pa_t_kernel(
                 issued[stage] = u + 1
 
         leads = (
-            (stage_products, -1, 0, -1),
-            (stage_quantise, 6, 0, 6),
-            (stage_fold, 2, 0, 2),
             (stage_transpose, 7, 0, 7),
             (stage_back, 0, 0, 0),
+            (stage_products, -1, 0, -1),
+            (stage_quantise, 6, 0, 6),
             (stage_sums, 1, 0, 1),
-            (stage_matmul_v, 1, 0, 1),
-            (stage_matmul_qk, 4, 0, 4),
             (stage_rstd_v, 0, 0, 0),
+            (stage_add, -2, 0, -2),
+            (stage_matmul_qk, 4, 0, 4),
+            (stage_fold, 2, 0, 2),
+            (stage_matmul_v, 1, 0, 1),
             (stage_copy, 7, 0, 7),
             (stage_gain_square, 3, 0, 3),
-            (stage_add, -2, 0, -2),
         )
         flags = set()
         for step in range(-8, N_UNITS + 2):

@@ -121,22 +121,22 @@ def tile_fluxattention_pa_t_kernel(
         x_tiles[4] = load_x(4)
         f_tiles[1] = load_f(1)
         x_tiles[5] = load_x(5)
-        f_tiles[3] = load_f(3)
         x_tiles[6] = load_x(6)
-        x_tiles[7] = load_x(7)
-        f_tiles[4] = load_f(4)
-        x_tiles[8] = load_x(8)
-        x_tiles[9] = load_x(9)
-        f_tiles[5] = load_f(5)
-        x_tiles[10] = load_x(10)
-        x_tiles[11] = load_x(11)
-        f_tiles[6] = load_f(6)
-        x_tiles[12] = load_x(12)
-        x_tiles[13] = load_x(13)
-        f_tiles[7] = load_f(7)
-        x_tiles[14] = load_x(14)
-        x_tiles[15] = load_x(15)
         f_tiles[2] = load_f(2)
+        x_tiles[7] = load_x(7)
+        x_tiles[8] = load_x(8)
+        f_tiles[3] = load_f(3)
+        x_tiles[9] = load_x(9)
+        x_tiles[10] = load_x(10)
+        f_tiles[4] = load_f(4)
+        x_tiles[11] = load_x(11)
+        x_tiles[12] = load_x(12)
+        f_tiles[5] = load_f(5)
+        x_tiles[13] = load_x(13)
+        x_tiles[14] = load_x(14)
+        f_tiles[6] = load_f(6)
+        x_tiles[15] = load_x(15)
+        f_tiles[7] = load_f(7)
 
         ident = const.tile([P, P], F32, name="ident")
         make_identity(nc, ident[:])

@@ -229,7 +229,7 @@ def tile_fluxattention_pa_t_kernel(
 
         def stage_quantise(u):
             c = u // 2
-            split = False
+            split = True
             if u % 2 == 0:
                 xc_new = cpool.tile([P, 512], U32, name="xc", align_bytes=64)
                 xs_new = cpool.tile([P, 512], U8, name="xs", align_bytes=64)
@@ -439,8 +439,6 @@ def tile_fluxattention_pa_t_kernel(
         for step in range(-8, N_UNITS + 2):
             for stage, first, ramp, lead in leads:
                 upto = step + (first if step < ramp else lead)
-                if stage == stage_quantise and upto % 2 == 0 and upto > -1:
-                    upto = upto - 1
                 advance(stage, upto)
             if issued.get(stage_transpose, 0) >= 2 and "gains" not in flags:
                 flags.add("gains")

from contextlib import ExitStack

import concourse.mybir as mybir
from concourse.masks import make_identity

FLOPS = 2 * 8192 * 512 * 384

F32 = mybir.dt.float32
BF16 = mybir.dt.bfloat16
U32 = mybir.dt.uint32
U8 = mybir.dt.uint8
FP8X4 = mybir.dt.float8_e4m3fn_x4
ALU = mybir.AluOpType
ACT = mybir.ActivationFunctionType

P = 128
EPS = 1e-6
GROUP_TILES = 8
N_GROUPS = 8
TEXT_GROUPS = 2
N_UNITS = 32
CHUNK_TILES = 4
N_CHUNKS = 16
SUM_COLS = 64


def tile_fluxattention_pa_t_kernel(
    tc,
    hidden_states,
    encoder_hidden_states,
    image_rotary_emb,
    W_iqkv,
    W_eqkv,
    qn_scale,
    kn_scale,
    eqn_scale,
    ekn_scale,
    out_0,
    out_1,
    out_2,
):
    nc = tc.nc
    x_img = hidden_states.flatten_outer_dims()
    x_txt = encoder_hidden_states.flatten_outer_dims()
    rot = image_rotary_emb.rearrange("l i f -> l (i f)")
    outs = [out_0.flatten_outer_dims(), out_1.flatten_outer_dims(), out_2.flatten_outer_dims()]

    with ExitStack() as ctx:
        ctx.enter_context(tc.manual_schedule())
        const = ctx.enter_context(tc.tile_pool(name="const", bufs=1))
        xpool = ctx.enter_context(tc.tile_pool(name="xpool", bufs=N_CHUNKS))
        fpool = ctx.enter_context(tc.tile_pool(name="fpool", bufs=N_GROUPS))
        gpool = ctx.enter_context(tc.tile_pool(name="gpool", bufs=4))
        cpool = ctx.enter_context(tc.tile_pool(name="cpool", bufs=9))
        zpool = ctx.enter_context(tc.tile_pool(name="zpool", bufs=6))
        ppool = ctx.enter_context(tc.tile_pool(name="ppool", bufs=3))
        opool = ctx.enter_context(tc.tile_pool(name="opool", bufs=6))
        stat = ctx.enter_context(tc.tile_pool(name="stat", bufs=4))
        tpsum = ctx.enter_context(tc.psum_pool(name="tpsum", bufs=2))
        ypsum = ctx.enter_context(tc.psum_pool(name="ypsum", bufs=2))
        zpsum = ctx.enter_context(tc.psum_pool(name="zpsum", bufs=2))
        vpsum = ctx.enter_context(tc.psum_pool(name="vpsum", bufs=2))

        def chunk_rows(dram, c, lo, hi):
            grp, half = divmod(c, 2)
            return dram[1024 * grp : 1024 * grp + 1024, :].rearrange("(p t) f -> p t f", t=GROUP_TILES)[
                :, 4 * half + lo : 4 * half + hi, :
            ]

        def load_w(w, name):
            raw = const.tile([P, 4, 384], BF16, name=name + "_raw")
            nc.sync.dma_start(out=raw[:], in_=w.rearrange("(p t) c -> p t c", t=4))
            return raw

        def load_x_part(xt, c, lo, hi):
            if c < 2 * TEXT_GROUPS:
                src, cc = x_txt, c
            else:
                src, cc = x_img, c - 2 * TEXT_GROUPS
            nc.sync.dma_start(out=xt[:, lo:hi, :], in_=chunk_rows(src, cc, lo, hi))

        def load_x(c):
            xt = xpool.tile([P, CHUNK_TILES, 512], BF16, name="x")
            load_x_part(xt, c, 0, CHUNK_TILES)
            return xt

        def load_f(grp):
            ft = fpool.tile([P, GROUP_TILES, 128], BF16, name="f")
            nc.sync.dma_start(
                out=ft[:],
                in_=rot[1024 * grp : 1024 * grp + 1024, :].rearrange("(p t) f -> p t f", t=GROUP_TILES),
            )
            return ft

        zeros = const.tile([P, 256], F32, name="zeros")
        nc.vector.memset(zeros[:], 0.0)

        gain_rows = const.tile([P, 128], BF16, name="gain_rows")
        nc.vector.memset(gain_rows[:], 0.0)

        def load_gains():
            for j, g in enumerate((eqn_scale, ekn_scale, qn_scale, kn_scale)):
                nc.sync.dma_start(
                    out=gain_rows[j // 2 : j // 2 + 1, 64 * (j % 2) : 64 * (j % 2) + 64], in_=g.rearrange("(o d) -> o d", o=1)
                )

        x_tiles = {}
        f_tiles = {}
        w_raw = {}
        x_first = xpool.tile([P, CHUNK_TILES, 512], BF16, name="x")
        x_tiles[0] = x_first
        load_x_part(x_first, 0, 0, 2)
        load_gains()
        w_raw[0] = load_w(W_eqkv, "we")
        load_x_part(x_first, 0, 2, 4)
        x_tiles[1] = load_x(1)
        x_tiles[2] = load_x(2)
        f_tiles[0] = load_f(0)
        x_tiles[3] = load_x(3)
        w_raw[1] = load_w(W_iqkv, "wi")
        x_tiles[4] = load_x(4)
        f_tiles[1] = load_f(1)
        x_tiles[5] = load_x(5)
        x_tiles[6] = load_x(6)
        f_tiles[2] = load_f(2)
        x_tiles[7] = load_x(7)
        x_tiles[8] = load_x(8)
        f_tiles[3] = load_f(3)
        x_tiles[9] = load_x(9)
        x_tiles[10] = load_x(10)
        f_tiles[4] = load_f(4)
        x_tiles[11] = load_x(11)
        x_tiles[12] = load_x(12)
        f_tiles[5] = load_f(5)
        x_tiles[13] = load_x(13)
        x_tiles[14] = load_x(14)
        f_tiles[6] = load_f(6)
        x_tiles[15] = load_x(15)
        f_tiles[7] = load_f(7)

        ident = const.tile([P, P], F32, name="ident")
        make_identity(nc, ident[:])
        ident_bf = const.tile([P, P], BF16, name="ident_bf")
        make_identity(nc, ident_bf[:])
        warm = const.tile([P, 1], F32, name="warm")
        nc.vector.memset(warm[:], 1.0)
        nc.scalar.activation(out=warm[:], in_=warm[:], func=ACT.Abs_reciprocal_sqrt)
        group_ones = const.tile([P, SUM_COLS], F32, name="group_ones")
        nc.vector.memset(group_ones[:], 0.0)
        for g in range(4):
            nc.vector.memset(group_ones[32 * g : 32 * g + 32, g : g + 1], 1.0)

        wg = {}
        w_q = {}

        def regroup_w(s, part, copy):
            name, raw = ("we", "wi")[s], w_raw[s]
            if s not in wg:
                grouped = const.tile([P, 384, 4], BF16, name=name + "_grouped", align_bytes=64)
                codes = const.tile([P, 384], U32, name=name + "_codes", align_bytes=64)
                scales = const.tile([P, 384], U8, name=name + "_scales", align_bytes=64)
                wg[s] = grouped
                w_q[s] = (codes, scales)
            grouped = wg[s]
            if part < 2:
                b = part
                copy(
                    out=grouped[:, 128 * b : 128 * b + 128, :],
                    in_=raw[:, :, 0:256].rearrange("p t (c b) -> p b c t", b=2)[:, b],
                )
            else:
                copy(out=grouped[:, 256:384, :], in_=raw[:, :, 256:384].rearrange("p t n -> p n t"))

        def quantise_w(s, part):
            codes, scales = w_q[s]
            lo, hi = ((0, 256), (256, 384))[part]
            nc.vector.quantize_mx(
                out=codes[:, lo:hi].bitcast(FP8X4),
                scales=scales[:, lo:hi],
                in_=wg[s][:, lo:hi, :].rearrange("p n t -> p (n t)"),
            )

        xt_tiles = {}
        xg_tiles = {}
        xq_tiles = {}
        yt_tiles = {}
        zt_tiles = {}
        sq_tiles = {}
        fold_tiles = {}
        z_tiles = {}
        vs_tiles = {}
        rstd_tiles = {}
        prod_tiles = {}
        o_tiles = {}
        vsb_tiles = {}

        def keep_clock(n):
            idle = zpsum.tile([P, 2, 2, 128], F32, name="z")
            nc.tensor.matmul(
                out=idle[:].rearrange("p a q c -> p (a q c)")[:, 0:n],
                lhsT=zeros[:, 0:128],
                rhs=zeros[:, 0:n],
                start=True,
                stop=True,
            )

        def stage_transpose(u):
            xw = x_tiles[u // 2][:].bitcast(F32)
            xt = tpsum.tile([P, 2, 2, 128], F32, name="xt")
            xt_tiles[u] = xt
            for a in range(2):
                for half in range(2):
                    nc.tensor.transpose(xt[:, a, half, :], xw[:, 2 * (u % 2) + a, half : 256 : 2], ident[:])
            if u < 3:
                keep_clock(256 if u < 2 else 128)

        def stage_copy(u):
            if u % 2 == 0:
                xg_new = gpool.tile([P, 2048], BF16, name="xg", align_bytes=64)
                xg_tiles[u // 2] = xg_new
            xg = xg_tiles[u // 2]
            copy = nc.scalar.copy if ("SSVVVVS"[u] if u < 7 else "SSSSV"[u % 5]) == "S" else nc.vector.tensor_copy
            copy(
                out=xg[:, 1024 * (u % 2) : 1024 * (u % 2) + 1024]
                .bitcast(F32)
                .rearrange("p (a r h) -> p a r h", a=2, r=128, h=2),
                in_=xt_tiles[u][:].rearrange("p a h r -> p a r h"),
            )

        def stage_quantise(u):
            c = u // 2
            split = True
            if u % 2 == 0:
                xc_new = cpool.tile([P, 512], U32, name="xc", align_bytes=64)
                xs_new = cpool.tile([P, 512], U8, name="xs", align_bytes=64)
                xq_tiles[c] = (xc_new, xs_new)
                if not split:
                    return
            xc, xs = xq_tiles[c]
            lo, hi = ((0, 256) if u % 2 == 0 else (256, 512)) if split else (0, 512)
            nc.vector.quantize_mx(out=xc[:, lo:hi].bitcast(FP8X4), scales=xs[:, lo:hi], in_=xg_tiles[c][:, 4 * lo : 4 * hi])

        def stage_matmul_qk(u):
            wc, ws = w_q[0 if u < 4 * TEXT_GROUPS else 1]
            xc, xs = xq_tiles[u // 2]
            yt = ypsum.tile([P, 2, 256], F32, name="yt")
            yt_tiles[u] = yt
            cols = slice(256 * (u % 2), 256 * (u % 2) + 256)
            for b in range(2):
                nc.tensor.matmul_mx(
                    out=yt[:, b, :],
                    lhsT=wc[:, 128 * b : 128 * b + 128].bitcast(FP8X4),
                    lhsT_scale=ws[:, 128 * b : 128 * b + 128],
                    rhs=xc[:, cols].bitcast(FP8X4),
                    rhs_scale=xs[:, cols],
                    start=True,
                    stop=True,
                )

        def stage_matmul_v(u):
            wc, ws = w_q[0 if u < 4 * TEXT_GROUPS else 1]
            xc, xs = xq_tiles[u // 2]
            vs = vs_tiles[u]
            for a in range(2):
                cols = slice(256 * (u % 2) + 128 * a, 256 * (u % 2) + 128 * a + 128)
                nc.tensor.matmul_mx(
                    out=vs[:, 128 * a : 128 * a + 128],
                    lhsT=xc[:, cols].bitcast(FP8X4),
                    lhsT_scale=xs[:, cols],
                    rhs=wc[:, 256:384].bitcast(FP8X4),
                    rhs_scale=ws[:, 256:384],
                    start=True,
                    stop=True,
                )

        def stage_gain_square(u):
            s = 0 if u < 4 * TEXT_GROUPS else 1
            zt = zpool.tile([P, 2, 256], F32, name="zt")
            zt_tiles[u] = zt
            sq = zpool.tile([P, 2, 256], F32, name="sq")
            sq_tiles[u] = sq
            nc.scalar.activation(
                out=sq[:].rearrange("p q r -> p (q r)"), in_=yt_tiles[u][:].rearrange("p q r -> p (q r)"), func=ACT.Square
            )
            for b in range(2):
                nc.scalar.activation(
                    out=zt[:, b, :], in_=yt_tiles[u][:, b, :], func=ACT.Copy, scale=gain_col[:, b, s : s + 1]
                )

        def folded(u):
            return int("0222222"[u % 7]) if 1 <= u < 31 else 0

        def stage_fold(u):
            if not folded(u):
                return
            fold = zpool.tile([P, 256], F32, name="fold")
            fold_tiles[u] = fold
            w = 128 * folded(u)
            nc.vector.tensor_tensor(out=fold[:, 0:w], in0=sq_tiles[u][:, 0, 0:w], in1=sq_tiles[u][:, 1, 0:w], op=ALU.add)

        def stage_back(u):
            z = zpsum.tile([P, 2, 2, 128], F32, name="z")
            z_tiles[u] = z
            for a in range(2):
                for b in range(2):
                    nc.tensor.transpose(
                        z[:, a].rearrange("p q (h b i) -> p b (q h) i", h=2, b=2)[:, b],
                        zt_tiles[u][:, b, 128 * a : 128 * a + 128],
                        ident[:],
                    )

        def stage_sums(u):
            vs = vpsum.tile([P, 256 + 2 * SUM_COLS], F32, name="vs")
            vs_tiles[u] = vs
            for a in range(2):
                if a < folded(u):
                    parts = [fold_tiles[u][:, 128 * a : 128 * a + 128]]
                else:
                    parts = [sq_tiles[u][:, b, 128 * a : 128 * a + 128] for b in range(2)]
                for k, part in enumerate(parts):
                    nc.tensor.matmul(
                        out=vs[:, 256 + SUM_COLS * a : 256 + SUM_COLS * (a + 1)],
                        lhsT=part,
                        rhs=group_ones[:],
                        start=(k == 0),
                        stop=(k == len(parts) - 1),
                    )

        def stage_rstd_v(u):
            rstd = stat.tile([P, 8], F32, name="rstd")
            nc.scalar.activation(
                out=rstd[:].rearrange("p (a g) -> p a g", g=4),
                in_=vs_tiles[u][:, 256 : 256 + 2 * SUM_COLS].rearrange("p (a n) -> p a n", n=SUM_COLS)[:, :, 0:4],
                func=ACT.Abs_reciprocal_sqrt,
                scale=1.0 / 64.0,
                bias=EPS,
            )
            rstd_tiles[u] = rstd
            if u % 2 == 0:
                vsb_new = opool.tile([P, CHUNK_TILES, 128], F32, name="vsb")
                vsb_tiles[u // 2] = vsb_new
            vsb = vsb_tiles[u // 2]
            nc.scalar.copy(
                out=vsb[:, 2 * (u % 2) : 2 * (u % 2) + 2, :].rearrange("p a c -> p (a c)"), in_=vs_tiles[u][:, 0:256]
            )
            if u % 2 == 1:
                nc.sync.dma_start(out=chunk_rows(outs[2], u // 2, 0, CHUNK_TILES), in_=vsb[:])

        def stage_products(u):
            grp, t0 = divmod(2 * u, GROUP_TILES)
            if u % 2 == 0:
                prod_new = ppool.tile([P, 2, CHUNK_TILES, 2, 128], F32, name="prod")
                prod_tiles[u // 2] = prod_new
            prod = prod_tiles[u // 2]
            for a in range(2):
                for g in range(4):
                    q, h = divmod(g, 2)
                    nc.vector.scalar_tensor_tensor(
                        out=prod[:, q, 2 * (u % 2) + a, h, :].rearrange("p (b i e) -> p b i e", b=2, e=2),
                        in0=z_tiles[u][:, a, q, 64 * h : 64 * h + 64]
                        .rearrange("p (b i) -> p b i", b=2)
                        .unsqueeze(3)
                        .to_broadcast([P, 2, 32, 2]),
                        scalar=rstd_tiles[u][:, 4 * a + g : 4 * a + g + 1],
                        in1=f_tiles[grp][:, t0 + a, :].rearrange("p (i e b) -> p b i e", e=2, b=2),
                        op0=ALU.mult,
                        op1=ALU.mult,
                    )

        def stage_add(u):
            c = u // 2
            if u % 2 == 0:
                o_new = opool.tile([P, 2, CHUNK_TILES, 128], F32, name="o")
                o_tiles[c] = o_new
            lo = 2 * (u % 2)
            pv = prod_tiles[c][:, :, lo : lo + 2].rearrange("p q t h (b c) -> p q (t h) b c", b=2)
            engine = nc.vector if u == N_UNITS - 1 else nc.gpsimd
            engine.tensor_tensor(
                out=o_tiles[c][:, :, lo : lo + 2, :].rearrange("p q t (h c) -> p q (t h) c", h=2),
                in0=pv[:, :, :, 0, :],
                in1=pv[:, :, :, 1, :],
                op=ALU.add,
            )
            if c == N_CHUNKS - 1:
                for q in range(2):
                    nc.sync.dma_start(out=chunk_rows(outs[q], c, lo, lo + 2), in_=o_tiles[c][:, q, lo : lo + 2, :])
            elif u % 2 == 1:
                for q in range(2):
                    nc.sync.dma_start(out=chunk_rows(outs[q], c, 0, CHUNK_TILES), in_=o_tiles[c][:, q])

        gain_perm = const.tile([P, 2, 128], BF16, name="gain_perm")
        for b in range(2):
            nc.vector.tensor_copy(
                out=gain_perm[:, b, :].rearrange("p (q h i) -> p q h i", q=2, h=2),
                in_=gain_rows[:]
                .rearrange("p (q i b) -> p b q i", q=2, b=2)[:, b]
                .unsqueeze(2)
                .to_broadcast([P, 2, 2, 32]),
            )
        gain_col = const.tile([P, 2, 2], F32, name="gain_col")

        def gain_columns():
            gain_ps = vpsum.tile([P, 2, 128], BF16, name="vs")
            for b in range(2):
                nc.tensor.transpose(gain_ps[:, b, :], gain_perm[:, b, :], ident_bf[:])
            nc.vector.tensor_copy(out=gain_col[:], in_=gain_ps[:, :, 0:2])

        for k in range(3):
            keep_clock(256)
        for part in range(3):
            regroup_w(0, part, nc.vector.tensor_copy)
        quantise_w(0, 0)
        quantise_w(0, 1)
        for part in range(3):
            regroup_w(1, part, nc.gpsimd.tensor_copy)

        issued = {}

        def advance(stage, upto):
            for u in range(issued.get(stage, 0), min(upto, N_UNITS - 1) + 1):
                stage(u)
                issued[stage] = u + 1

        leads = (
            (stage_transpose, 7, 0, 7),
            (stage_back, 0, 0, 0),
            (stage_products, -1, 0, -1),
            (stage_quantise, 6, 0, 6),
            (stage_sums, 1, 0, 1),
            (stage_rstd_v, 0, 0, 0),
            (stage_add, -2, 0, -2),
            (stage_matmul_qk, 4, 0, 4),
            (stage_fold, 2, 0, 2),
            (stage_matmul_v, 1, 0, 1),
            (stage_copy, 7, 0, 7),
            (stage_gain_square, 3, 0, 3),
        )
        flags = set()
        for step in range(-8, N_UNITS + 2):
            for stage, first, ramp, lead in leads:
                upto = step + (first if step < ramp else lead)
                advance(stage, upto)
            if issued.get(stage_transpose, 0) >= 2 and "gains" not in flags:
                flags.add("gains")
                gain_columns()
            if step == 1:
                quantise_w(1, 0)
                quantise_w(1, 1)
